import numpy as np
import ml_dtypes


def mxq(x, axis, fmt="e4m3"):
    dtype, down = {"e4m3": (ml_dtypes.float8_e4m3fn, 7), "e5m2": (ml_dtypes.float8_e5m2, 14)}[fmt]
    v = np.moveaxis(np.asarray(x, np.float32).astype(ml_dtypes.bfloat16).astype(np.float64), axis, -1)
    blocks = v.reshape(v.shape[:-1] + (-1, 32))
    amax = np.abs(blocks).max(-1, keepdims=True)
    byte = np.maximum(np.where(amax > 0, np.frexp(amax)[1] - 1 + 127, 0) - down, 1)
    scale = np.exp2(byte - 127.0)
    codes = (blocks / scale).astype(np.float32).astype(dtype).astype(np.float64)
    return np.moveaxis((codes * scale).reshape(v.shape), -1, axis)


WIDE = False


def mx_kscale(k):
    if not WIDE:
        return np.ones(k)
    levels = np.array([10, -10, 5, -5, 0])
    a = np.random.permutation(np.resize(levels, k // 512 * 4)).reshape(k // 512, 4)
    idx = np.arange(k)
    return np.exp2(a[idx // 512, idx % 128 // 32])


BF16 = ml_dtypes.bfloat16


def bf(x):
    return np.asarray(x, np.float32).astype(BF16)


def f64(x):
    return np.asarray(x).astype(np.float64)


B, T, D, BS = 1, 8192, 128, 8
N = T // BS


def compress(x):
    return x.reshape(B, N, BS, D).mean(axis=2)


def setup_inputs():
    t = mx_kscale(N)
    q = np.random.standard_normal((B, T, D)) * 2.0
    k = np.random.standard_normal((B, N, D))
    v = np.random.standard_normal((B, T, D)) * 2.0 * np.sqrt(BS)
    q[:, :, 0] = np.log(2.0) * np.sqrt(D)
    k[:, :, 0] -= np.log2(t)
    v *= np.repeat(t / t.min(), BS)[None, :, None]
    return {"queries": bf(q), "comp_k": bf(k), "values": bf(v),
            "gate_cmp": bf(np.random.random((B, T)))}


def reference(queries, comp_k, values, gate_cmp):
    comp_v = compress(f64(values))
    s = (f64(queries) @ f64(comp_k).transpose(0, 2, 1)) * D ** (-0.5)
    e = np.exp(s - s.max(-1, keepdims=True))
    comp_out = (mxq(e, 2, "e4m3") @ mxq(comp_v, 1, "e4m3")) / e.sum(-1, keepdims=True)
    return comp_out * f64(gate_cmp)[:, :, None]

@@ -1,0 +1,252 @@
+from contextlib import ExitStack
+
+import concourse.mybir as mybir
+from concourse.masks import make_identity
+
+BF16 = mybir.dt.bfloat16
+F32 = mybir.dt.float32
+U32 = mybir.dt.uint32
+U8 = mybir.dt.uint8
+FP8X4 = mybir.dt.float8_e4m3fn_x4
+ALU = mybir.AluOpType
+EXP = mybir.ActivationFunctionType.Exp
+X_AXIS = mybir.AxisListType.X
+
+P = 128
+T = 8192
+D = 128
+N = 1024
+BS = 8
+PACK = 4
+K_PASS = P * PACK
+PASSES = N // K_PASS
+CHUNKS = N // P
+TILES = T // P
+GROUP = 4
+GROUPS = TILES // GROUP
+Q_LOAD = 8
+SCALE = D ** -0.5
+
+SCALAR_COLS = 96
+
+SCORES_AHEAD = 1
+EXP_BEHIND = 1
+COPY_BEHIND = 2
+QUANTISE_BEHIND = 3
+Q_TRANSPOSE_AHEAD = 3
+MX_LAG = 1
+
+FLOPS = 2 * 2 * T * N * D
+
+
+def tile_nsa_pa_t_kernel(tc, queries, comp_k, values, gate_cmp, out):
+    nc = tc.nc
+    q_view = queries[0].rearrange("(p c) d -> p c d", c=TILES)
+    out_view = out[0].rearrange("(p c) d -> p c d", c=TILES)
+
+    with ExitStack() as ctx:
+        keep = ctx.enter_context(tc.tile_pool(name="keep", bufs=1))
+        pooling = ctx.enter_context(tc.tile_pool(name="pooling", bufs=1))
+        small = ctx.enter_context(tc.tile_pool(name="small", bufs=4))
+        stream = ctx.enter_context(tc.tile_pool(name="stream", bufs=3))
+        score_banks = ctx.enter_context(tc.psum_pool(name="score_banks", bufs=2 * PASSES))
+        flipped_banks = ctx.enter_context(tc.psum_pool(name="flipped_banks", bufs=2))
+        q_banks = ctx.enter_context(tc.psum_pool(name="q_banks", bufs=1))
+        out_banks = ctx.enter_context(tc.psum_pool(name="out_banks", bufs=1))
+        ctx.enter_context(tc.manual_schedule())
+
+        k_sb = keep.tile([P, PASSES, PACK, D], BF16)
+        nc.sync.dma_start(out=k_sb[:], in_=comp_k[0].rearrange("(g p j) d -> p g j d", g=PASSES, j=PACK))
+        q_sb = keep.tile([P, TILES, D], BF16)
+        nc.sync.dma_start(out=q_sb[:, 0:Q_LOAD, :], in_=q_view[:, 0:Q_LOAD, :])
+        gate_sb = keep.tile([P, TILES], BF16)
+        nc.sync.dma_start(out=gate_sb[:], in_=gate_cmp[0].rearrange("(p c) -> p c", c=TILES))
+        v_sb = keep.tile([P, PASSES, PACK * BS, D], BF16)
+        v_view = values[0].rearrange("(g p r) d -> p g r d", g=PASSES, r=PACK * BS)
+        for g in range(PASSES):
+            nc.sync.dma_start(out=v_sb[:, g], in_=v_view[:, g])
+        for first in range(Q_LOAD, TILES, Q_LOAD):
+            nc.sync.dma_start(out=q_sb[:, first : first + Q_LOAD, :], in_=q_view[:, first : first + Q_LOAD, :])
+
+        identity = keep.tile([P, P], BF16)
+        make_identity(nc, identity[:])
+        warm = keep.tile([P, 1], F32)
+        nc.vector.memset(warm[:], 0.0)
+        nc.scalar.activation(out=warm[:], in_=warm[:], func=EXP)
+
+        kT_ps = flipped_banks.tile([P, CHUNKS, P], BF16, tag="flipped")
+        for g in range(PASSES):
+            for j in range(PACK):
+                nc.tensor.transpose(kT_ps[:, g * PACK + j, :], k_sb[:, g, j, :], identity[:])
+        kT_sb = keep.tile([P, N], BF16)
+        nc.vector.tensor_copy(out=kT_sb[:], in_=kT_ps[:].rearrange("p a n -> p (a n)"))
+
+        v_grouped = keep.tile([P, PASSES, D, PACK], BF16, align_bytes=64)
+        for g in range(PASSES):
+            rows8 = v_sb[:, g].rearrange("p (j i) d -> p j (i d)", i=BS)
+            rows4 = pooling.tile([P, PACK, 4 * D], F32)
+            nc.gpsimd.tensor_tensor(out=rows4[:], in0=rows8[:, :, 0 : 4 * D], in1=rows8[:, :, 4 * D : 8 * D], op=ALU.add)
+            rows2 = pooling.tile([P, PACK, 2 * D], F32)
+            nc.gpsimd.tensor_tensor(out=rows2[:], in0=rows4[:, :, 0 : 2 * D], in1=rows4[:, :, 2 * D : 4 * D], op=ALU.add)
+            rows1 = pooling.tile([P, PACK, D], F32)
+            nc.gpsimd.tensor_tensor(out=rows1[:], in0=rows2[:, :, 0:D], in1=rows2[:, :, D : 2 * D], op=ALU.add)
+            nc.gpsimd.tensor_scalar(
+                out=v_grouped[:, g],
+                in0=rows1[:].rearrange("p j d -> p d j"),
+                scalar1=1.0 / BS,
+                scalar2=0.0,
+                op0=ALU.mult,
+                op1=ALU.add,
+            )
+        v_codes = keep.tile([P, PASSES, D], U32, align_bytes=64)
+        v_scales = keep.tile([P, PASSES, D], U8, align_bytes=64)
+
+        e_codes = keep.tile([P, TILES, PASSES * P], U32, align_bytes=64)
+        e_scales = keep.tile([P, TILES, PASSES * P], U8, align_bytes=64)
+        row_sums = keep.tile([P, TILES, PASSES], F32)
+        qT_of = {}
+        scores_of = {}
+        neg_max_of = {}
+        e_of = {}
+        flipped_of = {}
+        grouped_of = {}
+        out_of = {}
+
+        def exists(tile_index):
+            return 0 <= tile_index < TILES
+
+        def transpose_queries(group):
+            qT_ps = q_banks.tile([P, GROUP, P], BF16)
+            for c in range(GROUP):
+                nc.tensor.transpose(qT_ps[:, c, :], q_sb[:, group * GROUP + c, :], identity[:])
+            qT = stream.tile([P, GROUP, P], BF16)
+            nc.vector.tensor_copy(out=qT[:], in_=qT_ps[:])
+            qT_of[group] = qT
+
+        def scores_and_transposes(score_tile, flip_tile):
+            if exists(flip_tile):
+                flipped = flipped_banks.tile([P, CHUNKS, P], BF16, tag="flipped")
+                flipped_of[flip_tile] = flipped
+            for g in range(PASSES):
+                if exists(score_tile):
+                    scores = score_banks.tile([P, K_PASS], F32)
+                    nc.tensor.matmul(
+                        out=scores[:],
+                        lhsT=qT_of[score_tile // GROUP][:, score_tile % GROUP, :],
+                        rhs=kT_sb[:, g * K_PASS : (g + 1) * K_PASS],
+                        start=True,
+                        stop=True,
+                    )
+                    scores_of[(score_tile, g)] = scores
+                if exists(flip_tile):
+                    for a in range(g * PACK, (g + 1) * PACK):
+                        nc.tensor.transpose(
+                            flipped_of[flip_tile][:, a, :], e_of[flip_tile][:, a * P : (a + 1) * P], identity[:]
+                        )
+
+        def row_maximum(i):
+            bank_max = small.tile([P, PASSES], F32)
+            for g in range(PASSES):
+                nc.vector.tensor_reduce(out=bank_max[:, g : g + 1], in_=scores_of[(i, g)][:], axis=X_AXIS, op=ALU.max)
+            neg_max = small.tile([P, 1], F32)
+            nc.vector.tensor_scalar(
+                out=neg_max[:],
+                in0=bank_max[:, 0:1],
+                scalar1=bank_max[:, 1:2],
+                scalar2=-SCALE,
+                op0=ALU.max,
+                op1=ALU.mult,
+            )
+            neg_max_of[i] = neg_max
+
+        def exponentials(i):
+            e = stream.tile([P, N], BF16)
+            for g in range(PASSES):
+                nc.scalar.activation(
+                    out=e[:, g * K_PASS : (g + 1) * K_PASS],
+                    in_=scores_of[(i, g)][:],
+                    func=EXP,
+                    bias=neg_max_of[i][:],
+                    scale=SCALE,
+                    accum_out=row_sums[:, i, g : g + 1],
+                )
+            e_of[i] = e
+
+        def flipped_columns(i, columns):
+            return flipped_of[i][:, :, columns].rearrange("p (g j) t -> p g t j", j=PACK)
+
+        def copy_out_on_vector(i):
+            grouped = stream.tile([P, PASSES, P, PACK], BF16, align_bytes=64)
+            grouped_of[i] = grouped
+            columns = slice(SCALAR_COLS, P)
+            nc.vector.tensor_copy(out=grouped[:, :, columns, :], in_=flipped_columns(i, columns))
+
+        def copy_out_on_scalar(i):
+            columns = slice(0, SCALAR_COLS)
+            nc.scalar.copy(out=grouped_of[i][:, :, columns, :], in_=flipped_columns(i, columns))
+
+        def quantise(i):
+            nc.vector.quantize_mx(
+                out=e_codes[:, i, :].bitcast(FP8X4),
+                scales=e_scales[:, i, :],
+                in_=grouped_of[i][:].rearrange("p g t j -> p (g t j)"),
+            )
+
+        def weighted_sums(group):
+            out_ps = out_banks.tile([P, GROUP, D], F32)
+            for c in range(GROUP):
+                i = group * GROUP + c
+                for g in range(PASSES):
+                    nc.tensor.matmul_mx(
+                        out=out_ps[:, c, :],
+                        lhsT=e_codes[:, i, g * P : (g + 1) * P].bitcast(FP8X4),
+                        lhsT_scale=e_scales[:, i, g * P : (g + 1) * P],
+                        rhs=v_codes[:, g, :].bitcast(FP8X4),
+                        rhs_scale=v_scales[:, g, :],
+                        start=(g == 0),
+                        stop=(g == PASSES - 1),
+                    )
+            out_of[group] = out_ps
+
+        def finish(group):
+            tiles = slice(group * GROUP, (group + 1) * GROUP)
+            factor = small.tile([P, GROUP], F32)
+            nc.vector.tensor_reduce(out=factor[:], in_=row_sums[:, tiles, :], axis=X_AXIS, op=ALU.add)
+            nc.vector.reciprocal(out=factor[:], in_=factor[:])
+            nc.vector.tensor_tensor(out=factor[:], in0=factor[:], in1=gate_sb[:, tiles], op=ALU.mult)
+            out_sb = stream.tile([P, GROUP, D], F32)
+            nc.vector.tensor_tensor(
+                out=out_sb[:],
+                in0=out_of[group][:],
+                in1=factor[:].unsqueeze(2).to_broadcast([P, GROUP, D]),
+                op=ALU.mult,
+            )
+            nc.sync.dma_start(out=out_view[:, tiles, :], in_=out_sb[:])
+
+        mx_offset = GROUP + QUANTISE_BEHIND + GROUP * MX_LAG
+        for step in range(-Q_TRANSPOSE_AHEAD, GROUP * (GROUPS - 1) + mx_offset + 1):
+            mx_group, mx_rest = divmod(step - mx_offset, GROUP)
+            mx_due = mx_rest == 0 and 0 <= mx_group < GROUPS
+            if mx_due and mx_group == 0:
+                nc.vector.quantize_mx(
+                    out=v_codes[:].rearrange("p g d -> p (g d)").bitcast(FP8X4),
+                    scales=v_scales[:].rearrange("p g d -> p (g d)"),
+                    in_=v_grouped[:].rearrange("p g d j -> p (g d j)"),
+                )
+            if mx_due:
+                weighted_sums(mx_group)
+            if exists(step - COPY_BEHIND):
+                copy_out_on_vector(step - COPY_BEHIND)
+            if exists(step - EXP_BEHIND):
+                exponentials(step - EXP_BEHIND)
+            scores_and_transposes(step + SCORES_AHEAD, step - EXP_BEHIND)
+            if exists(step):
+                row_maximum(step)
+            if exists(step - COPY_BEHIND):
+                copy_out_on_scalar(step - COPY_BEHIND)
+            if exists(step - QUANTISE_BEHIND):
+                quantise(step - QUANTISE_BEHIND)
+            if exists(step + Q_TRANSPOSE_AHEAD) and (step + Q_TRANSPOSE_AHEAD) % GROUP == 0:
+                transpose_queries((step + Q_TRANSPOSE_AHEAD) // GROUP)
+            if mx_due:
+                finish(mx_group)

@@ -20,20 +20,21 @@ BS = 8
 PACK = 4
 K_PASS = P * PACK
 PASSES = N // K_PASS
-CHUNKS = N // P
 TILES = T // P
 GROUP = 4
 GROUPS = TILES // GROUP
 Q_LOAD = 8
 SCALE = D ** -0.5
 
-SCALAR_COLS = 96
+VECTOR_COPY_EVERY = 4
 
-SCORES_AHEAD = 1
-EXP_BEHIND = 1
-COPY_BEHIND = 2
-QUANTISE_BEHIND = 3
-Q_TRANSPOSE_AHEAD = 3
+SCORE_BANKS = 5
+
+MAX_AHEAD = 1
+COPY_BEHIND = 1
+QUANTISE_BEHIND = 2
+Q_TRANSPOSE_AHEAD = 5
+Q_COPY_AHEAD = 4
 MX_LAG = 1
 
 FLOPS = 2 * 2 * T * N * D
@@ -49,11 +50,9 @@ def tile_nsa_pa_t_kernel(tc, queries, comp_k, values, gate_cmp, out):
         pooling = ctx.enter_context(tc.tile_pool(name="pooling", bufs=1))
         small = ctx.enter_context(tc.tile_pool(name="small", bufs=4))
         stream = ctx.enter_context(tc.tile_pool(name="stream", bufs=3))
-        score_banks = ctx.enter_context(tc.psum_pool(name="score_banks", bufs=2 * PASSES))
-        flipped_banks = ctx.enter_context(tc.psum_pool(name="flipped_banks", bufs=2))
-        q_banks = ctx.enter_context(tc.psum_pool(name="q_banks", bufs=1))
-        out_banks = ctx.enter_context(tc.psum_pool(name="out_banks", bufs=1))
-        ctx.enter_context(tc.manual_schedule())
+        score_banks = ctx.enter_context(tc.psum_pool(name="score_banks", bufs=SCORE_BANKS))
+        flipped_banks = ctx.enter_context(tc.psum_pool(name="flipped_banks", bufs=PASSES))
+        shared_bank = ctx.enter_context(tc.psum_pool(name="shared_bank", bufs=1))
 
         k_sb = keep.tile([P, PASSES, PACK, D], BF16)
         nc.sync.dma_start(out=k_sb[:], in_=comp_k[0].rearrange("(g p j) d -> p g j d", g=PASSES, j=PACK))
@@ -74,36 +73,30 @@ def tile_nsa_pa_t_kernel(tc, queries, comp_k, values, gate_cmp, out):
         nc.vector.memset(warm[:], 0.0)
         nc.scalar.activation(out=warm[:], in_=warm[:], func=EXP)
 
-        kT_ps = flipped_banks.tile([P, CHUNKS, P], BF16, tag="flipped")
-        for g in range(PASSES):
-            for j in range(PACK):
-                nc.tensor.transpose(kT_ps[:, g * PACK + j, :], k_sb[:, g, j, :], identity[:])
         kT_sb = keep.tile([P, N], BF16)
-        nc.vector.tensor_copy(out=kT_sb[:], in_=kT_ps[:].rearrange("p a n -> p (a n)"))
+        for g in range(PASSES):
+            kT_ps = flipped_banks.tile([P, PACK, P], BF16, tag="flipped")
+            for j in range(PACK):
+                nc.tensor.transpose(kT_ps[:, j, :], k_sb[:, g, j, :], identity[:])
+            nc.vector.tensor_copy(
+                out=kT_sb[:, g * K_PASS : (g + 1) * K_PASS], in_=kT_ps[:].rearrange("p j n -> p (j n)")
+            )
 
-        v_grouped = keep.tile([P, PASSES, D, PACK], BF16, align_bytes=64)
+        block_sums = keep.tile([P, PASSES, PACK, D], F32)
         for g in range(PASSES):
             rows8 = v_sb[:, g].rearrange("p (j i) d -> p j (i d)", i=BS)
             rows4 = pooling.tile([P, PACK, 4 * D], F32)
             nc.gpsimd.tensor_tensor(out=rows4[:], in0=rows8[:, :, 0 : 4 * D], in1=rows8[:, :, 4 * D : 8 * D], op=ALU.add)
             rows2 = pooling.tile([P, PACK, 2 * D], F32)
             nc.gpsimd.tensor_tensor(out=rows2[:], in0=rows4[:, :, 0 : 2 * D], in1=rows4[:, :, 2 * D : 4 * D], op=ALU.add)
-            rows1 = pooling.tile([P, PACK, D], F32)
-            nc.gpsimd.tensor_tensor(out=rows1[:], in0=rows2[:, :, 0:D], in1=rows2[:, :, D : 2 * D], op=ALU.add)
-            nc.gpsimd.tensor_scalar(
-                out=v_grouped[:, g],
-                in0=rows1[:].rearrange("p j d -> p d j"),
-                scalar1=1.0 / BS,
-                scalar2=0.0,
-                op0=ALU.mult,
-                op1=ALU.add,
-            )
+            nc.gpsimd.tensor_tensor(out=block_sums[:, g], in0=rows2[:, :, 0:D], in1=rows2[:, :, D : 2 * D], op=ALU.add)
         v_codes = keep.tile([P, PASSES, D], U32, align_bytes=64)
         v_scales = keep.tile([P, PASSES, D], U8, align_bytes=64)
 
         e_codes = keep.tile([P, TILES, PASSES * P], U32, align_bytes=64)
         e_scales = keep.tile([P, TILES, PASSES * P], U8, align_bytes=64)
         row_sums = keep.tile([P, TILES, PASSES], F32)
+        qT_ps_of = {}
         qT_of = {}
         scores_of = {}
         neg_max_of = {}
@@ -116,33 +109,28 @@ def tile_nsa_pa_t_kernel(tc, queries, comp_k, values, gate_cmp, out):
             return 0 <= tile_index < TILES
 
         def transpose_queries(group):
-            qT_ps = q_banks.tile([P, GROUP, P], BF16)
+            qT_ps = shared_bank.tile([P, GROUP, P], BF16, tag="shared")
             for c in range(GROUP):
                 nc.tensor.transpose(qT_ps[:, c, :], q_sb[:, group * GROUP + c, :], identity[:])
+            qT_ps_of[group] = qT_ps
+
+        def copy_queries(group):
             qT = stream.tile([P, GROUP, P], BF16)
-            nc.vector.tensor_copy(out=qT[:], in_=qT_ps[:])
+            nc.vector.tensor_copy(out=qT[:], in_=qT_ps_of[group][:])
             qT_of[group] = qT
 
-        def scores_and_transposes(score_tile, flip_tile):
-            if exists(flip_tile):
-                flipped = flipped_banks.tile([P, CHUNKS, P], BF16, tag="flipped")
-                flipped_of[flip_tile] = flipped
-            for g in range(PASSES):
-                if exists(score_tile):
-                    scores = score_banks.tile([P, K_PASS], F32)
-                    nc.tensor.matmul(
-                        out=scores[:],
-                        lhsT=qT_of[score_tile // GROUP][:, score_tile % GROUP, :],
-                        rhs=kT_sb[:, g * K_PASS : (g + 1) * K_PASS],
-                        start=True,
-                        stop=True,
-                    )
-                    scores_of[(score_tile, g)] = scores
-                if exists(flip_tile):
-                    for a in range(g * PACK, (g + 1) * PACK):
-                        nc.tensor.transpose(
-                            flipped_of[flip_tile][:, a, :], e_of[flip_tile][:, a * P : (a + 1) * P], identity[:]
-                        )
+        def scores(half):
+            i, g = divmod(half, PASSES)
+            if exists(i):
+                bank = score_banks.tile([P, K_PASS], F32)
+                nc.tensor.matmul(
+                    out=bank[:],
+                    lhsT=qT_of[i // GROUP][:, i % GROUP, :],
+                    rhs=kT_sb[:, g * K_PASS : (g + 1) * K_PASS],
+                    start=True,
+                    stop=True,
+                )
+                scores_of[(i, g)] = bank
 
         def row_maximum(i):
             bank_max = small.tile([P, PASSES], F32)
@@ -159,31 +147,35 @@ def tile_nsa_pa_t_kernel(tc, queries, comp_k, values, gate_cmp, out):
             )
             neg_max_of[i] = neg_max
 
-        def exponentials(i):
-            e = stream.tile([P, N], BF16)
-            for g in range(PASSES):
-                nc.scalar.activation(
-                    out=e[:, g * K_PASS : (g + 1) * K_PASS],
-                    in_=scores_of[(i, g)][:],
-                    func=EXP,
-                    bias=neg_max_of[i][:],
-                    scale=SCALE,
-                    accum_out=row_sums[:, i, g : g + 1],
-                )
-            e_of[i] = e
+        def exponential(i, g):
+            if g == 0:
+                e = stream.tile([P, N], BF16)
+                e_of[i] = e
+            nc.scalar.activation(
+                out=e_of[i][:, g * K_PASS : (g + 1) * K_PASS],
+                in_=scores_of[(i, g)][:],
+                func=EXP,
+                bias=neg_max_of[i][:],
+                scale=SCALE,
+                accum_out=row_sums[:, i, g : g + 1],
+            )
 
-        def flipped_columns(i, columns):
-            return flipped_of[i][:, :, columns].rearrange("p (g j) t -> p g t j", j=PACK)
+        def transpose_e(i, g):
+            flipped = flipped_banks.tile([P, PACK, P], BF16, tag="flipped")
+            for j in range(PACK):
+                a = g * PACK + j
+                nc.tensor.transpose(flipped[:, j, :], e_of[i][:, a * P : (a + 1) * P], identity[:])
+            flipped_of[(i, g)] = flipped
 
-        def copy_out_on_vector(i):
-            grouped = stream.tile([P, PASSES, P, PACK], BF16, align_bytes=64)
-            grouped_of[i] = grouped
-            columns = slice(SCALAR_COLS, P)
-            nc.vector.tensor_copy(out=grouped[:, :, columns, :], in_=flipped_columns(i, columns))
-
-        def copy_out_on_scalar(i):
-            columns = slice(0, SCALAR_COLS)
-            nc.scalar.copy(out=grouped_of[i][:, :, columns, :], in_=flipped_columns(i, columns))
+        def copy_out(i, g):
+            if g == 0:
+                grouped = stream.tile([P, PASSES, P, PACK], BF16, align_bytes=64)
+                grouped_of[i] = grouped
+            words = flipped_of[(i, g)][:].rearrange("p j t -> p t j")
+            if (PASSES * i + g) % VECTOR_COPY_EVERY == VECTOR_COPY_EVERY - 1:
+                nc.vector.tensor_copy(out=grouped_of[i][:, g], in_=words)
+            else:
+                nc.scalar.copy(out=grouped_of[i][:, g], in_=words)
 
         def quantise(i):
             nc.vector.quantize_mx(
@@ -193,7 +185,7 @@ def tile_nsa_pa_t_kernel(tc, queries, comp_k, values, gate_cmp, out):
             )
 
         def weighted_sums(group):
-            out_ps = out_banks.tile([P, GROUP, D], F32)
+            out_ps = shared_bank.tile([P, GROUP, D], F32, tag="shared")
             for c in range(GROUP):
                 i = group * GROUP + c
                 for g in range(PASSES):
@@ -228,6 +220,16 @@ def tile_nsa_pa_t_kernel(tc, queries, comp_k, values, gate_cmp, out):
             mx_group, mx_rest = divmod(step - mx_offset, GROUP)
             mx_due = mx_rest == 0 and 0 <= mx_group < GROUPS
             if mx_due and mx_group == 0:
+                v_grouped = stream.tile([P, PASSES, D, PACK], BF16, align_bytes=64, tag="grouped")
+                for g in range(PASSES):
+                    nc.gpsimd.tensor_scalar(
+                        out=v_grouped[:, g],
+                        in0=block_sums[:, g].rearrange("p j d -> p d j"),
+                        scalar1=1.0 / BS,
+                        scalar2=0.0,
+                        op0=ALU.mult,
+                        op1=ALU.add,
+                    )
                 nc.vector.quantize_mx(
                     out=v_codes[:].rearrange("p g d -> p (g d)").bitcast(FP8X4),
                     scales=v_scales[:].rearrange("p g d -> p (g d)"),
@@ -235,17 +237,21 @@ def tile_nsa_pa_t_kernel(tc, queries, comp_k, values, gate_cmp, out):
                 )
             if mx_due:
                 weighted_sums(mx_group)
-            if exists(step - COPY_BEHIND):
-                copy_out_on_vector(step - COPY_BEHIND)
-            if exists(step - EXP_BEHIND):
-                exponentials(step - EXP_BEHIND)
-            scores_and_transposes(step + SCORES_AHEAD, step - EXP_BEHIND)
-            if exists(step):
-                row_maximum(step)
-            if exists(step - COPY_BEHIND):
-                copy_out_on_scalar(step - COPY_BEHIND)
+            if exists(step + MAX_AHEAD):
+                row_maximum(step + MAX_AHEAD)
+            for g in range(PASSES):
+                if exists(step):
+                    exponential(step, g)
+                scores(PASSES * step + g + SCORE_BANKS)
+            for g in range(PASSES):
+                if exists(step - COPY_BEHIND):
+                    copy_out(step - COPY_BEHIND, g)
+                if exists(step):
+                    transpose_e(step, g)
             if exists(step - QUANTISE_BEHIND):
                 quantise(step - QUANTISE_BEHIND)
+            if exists(step + Q_COPY_AHEAD) and (step + Q_COPY_AHEAD) % GROUP == 0:
+                copy_queries((step + Q_COPY_AHEAD) // GROUP)
             if exists(step + Q_TRANSPOSE_AHEAD) and (step + Q_TRANSPOSE_AHEAD) % GROUP == 0:
                 transpose_queries((step + Q_TRANSPOSE_AHEAD) // GROUP)
             if mx_due:

@@ -29,6 +29,7 @@ SCALE = D ** -0.5
 VECTOR_COPY_EVERY = 4
 
 SCORE_BANKS = 5
+RING_BANKS = 3
 
 MAX_AHEAD = 1
 COPY_BEHIND = 1
@@ -51,8 +52,7 @@ def tile_nsa_pa_t_kernel(tc, queries, comp_k, values, gate_cmp, out):
         small = ctx.enter_context(tc.tile_pool(name="small", bufs=4))
         stream = ctx.enter_context(tc.tile_pool(name="stream", bufs=3))
         score_banks = ctx.enter_context(tc.psum_pool(name="score_banks", bufs=SCORE_BANKS))
-        flipped_banks = ctx.enter_context(tc.psum_pool(name="flipped_banks", bufs=PASSES))
-        shared_bank = ctx.enter_context(tc.psum_pool(name="shared_bank", bufs=1))
+        ring_banks = ctx.enter_context(tc.psum_pool(name="ring_banks", bufs=RING_BANKS))
 
         k_sb = keep.tile([P, PASSES, PACK, D], BF16)
         nc.sync.dma_start(out=k_sb[:], in_=comp_k[0].rearrange("(g p j) d -> p g j d", g=PASSES, j=PACK))
@@ -75,7 +75,7 @@ def tile_nsa_pa_t_kernel(tc, queries, comp_k, values, gate_cmp, out):
 
         kT_sb = keep.tile([P, N], BF16)
         for g in range(PASSES):
-            kT_ps = flipped_banks.tile([P, PACK, P], BF16, tag="flipped")
+            kT_ps = ring_banks.tile([P, PACK, P], BF16, tag="ring")
             for j in range(PACK):
                 nc.tensor.transpose(kT_ps[:, j, :], k_sb[:, g, j, :], identity[:])
             nc.vector.tensor_copy(
@@ -109,7 +109,7 @@ def tile_nsa_pa_t_kernel(tc, queries, comp_k, values, gate_cmp, out):
             return 0 <= tile_index < TILES
 
         def transpose_queries(group):
-            qT_ps = shared_bank.tile([P, GROUP, P], BF16, tag="shared")
+            qT_ps = ring_banks.tile([P, GROUP, P], BF16, tag="ring")
             for c in range(GROUP):
                 nc.tensor.transpose(qT_ps[:, c, :], q_sb[:, group * GROUP + c, :], identity[:])
             qT_ps_of[group] = qT_ps
@@ -119,8 +119,8 @@ def tile_nsa_pa_t_kernel(tc, queries, comp_k, values, gate_cmp, out):
             nc.vector.tensor_copy(out=qT[:], in_=qT_ps_of[group][:])
             qT_of[group] = qT
 
-        def scores(half):
-            i, g = divmod(half, PASSES)
+        def scores(bank_number):
+            i, g = divmod(bank_number, PASSES)
             if exists(i):
                 bank = score_banks.tile([P, K_PASS], F32)
                 nc.tensor.matmul(
@@ -161,21 +161,20 @@ def tile_nsa_pa_t_kernel(tc, queries, comp_k, values, gate_cmp, out):
             )
 
         def transpose_e(i, g):
-            flipped = flipped_banks.tile([P, PACK, P], BF16, tag="flipped")
-            for j in range(PACK):
-                a = g * PACK + j
-                nc.tensor.transpose(flipped[:, j, :], e_of[i][:, a * P : (a + 1) * P], identity[:])
-            flipped_of[(i, g)] = flipped
-
-        def copy_out(i, g):
             if g == 0:
-                grouped = stream.tile([P, PASSES, P, PACK], BF16, align_bytes=64)
-                grouped_of[i] = grouped
-            words = flipped_of[(i, g)][:].rearrange("p j t -> p t j")
-            if (PASSES * i + g) % VECTOR_COPY_EVERY == VECTOR_COPY_EVERY - 1:
-                nc.vector.tensor_copy(out=grouped_of[i][:, g], in_=words)
+                flipped = ring_banks.tile([P, PASSES * PACK, P], BF16, tag="ring")
+                flipped_of[i] = flipped
+            for a in range(g * PACK, (g + 1) * PACK):
+                nc.tensor.transpose(flipped_of[i][:, a, :], e_of[i][:, a * P : (a + 1) * P], identity[:])
+
+        def copy_out(i):
+            grouped = stream.tile([P, PASSES, P, PACK], BF16, align_bytes=64)
+            words = flipped_of[i][:].rearrange("p (g j) t -> p g t j", j=PACK)
+            if i % VECTOR_COPY_EVERY == VECTOR_COPY_EVERY - 1:
+                nc.vector.tensor_copy(out=grouped[:], in_=words)
             else:
-                nc.scalar.copy(out=grouped_of[i][:, g], in_=words)
+                nc.scalar.copy(out=grouped[:], in_=words)
+            grouped_of[i] = grouped
 
         def quantise(i):
             nc.vector.quantize_mx(
@@ -185,7 +184,7 @@ def tile_nsa_pa_t_kernel(tc, queries, comp_k, values, gate_cmp, out):
             )
 
         def weighted_sums(group):
-            out_ps = shared_bank.tile([P, GROUP, D], F32, tag="shared")
+            out_ps = ring_banks.tile([P, GROUP, D], F32, tag="ring")
             for c in range(GROUP):
                 i = group * GROUP + c
                 for g in range(PASSES):
@@ -235,19 +234,15 @@ def tile_nsa_pa_t_kernel(tc, queries, comp_k, values, gate_cmp, out):
                     scales=v_scales[:].rearrange("p g d -> p (g d)"),
                     in_=v_grouped[:].rearrange("p g d j -> p (g d j)"),
                 )
-            if mx_due:
-                weighted_sums(mx_group)
             if exists(step + MAX_AHEAD):
                 row_maximum(step + MAX_AHEAD)
             for g in range(PASSES):
                 if exists(step):
                     exponential(step, g)
-                scores(PASSES * step + g + SCORE_BANKS)
-            for g in range(PASSES):
-                if exists(step - COPY_BEHIND):
-                    copy_out(step - COPY_BEHIND, g)
-                if exists(step):
                     transpose_e(step, g)
+                scores(PASSES * step + g + SCORE_BANKS)
+            if exists(step - COPY_BEHIND):
+                copy_out(step - COPY_BEHIND)
             if exists(step - QUANTISE_BEHIND):
                 quantise(step - QUANTISE_BEHIND)
             if exists(step + Q_COPY_AHEAD) and (step + Q_COPY_AHEAD) % GROUP == 0:
@@ -255,4 +250,5 @@ def tile_nsa_pa_t_kernel(tc, queries, comp_k, values, gate_cmp, out):
             if exists(step + Q_TRANSPOSE_AHEAD) and (step + Q_TRANSPOSE_AHEAD) % GROUP == 0:
                 transpose_queries((step + Q_TRANSPOSE_AHEAD) // GROUP)
             if mx_due:
+                weighted_sums(mx_group)
                 finish(mx_group)

@@ -26,7 +26,7 @@ GROUPS = TILES // GROUP
 Q_LOAD = 8
 SCALE = D ** -0.5
 
-VECTOR_COPY_EVERY = 4
+SCALAR_COLS = 88
 
 SCORE_BANKS = 5
 RING_BANKS = 3
@@ -170,10 +170,8 @@ def tile_nsa_pa_t_kernel(tc, queries, comp_k, values, gate_cmp, out):
         def copy_out(i):
             grouped = stream.tile([P, PASSES, P, PACK], BF16, align_bytes=64)
             words = flipped_of[i][:].rearrange("p (g j) t -> p g t j", j=PACK)
-            if i % VECTOR_COPY_EVERY == VECTOR_COPY_EVERY - 1:
-                nc.vector.tensor_copy(out=grouped[:], in_=words)
-            else:
-                nc.scalar.copy(out=grouped[:], in_=words)
+            nc.scalar.copy(out=grouped[:, :, 0:SCALAR_COLS, :], in_=words[:, :, 0:SCALAR_COLS, :])
+            nc.vector.tensor_copy(out=grouped[:, :, SCALAR_COLS:P, :], in_=words[:, :, SCALAR_COLS:P, :])
             grouped_of[i] = grouped
 
         def quantise(i):

@@ -26,7 +26,6 @@ GROUPS = TILES // GROUP
 Q_LOAD = 8
 SCALE = D ** -0.5
 
-SCALAR_COLS = 88
 
 SCORE_BANKS = 5
 RING_BANKS = 3
@@ -50,7 +49,7 @@ def tile_nsa_pa_t_kernel(tc, queries, comp_k, values, gate_cmp, out):
         keep = ctx.enter_context(tc.tile_pool(name="keep", bufs=1))
         pooling = ctx.enter_context(tc.tile_pool(name="pooling", bufs=1))
         small = ctx.enter_context(tc.tile_pool(name="small", bufs=4))
-        stream = ctx.enter_context(tc.tile_pool(name="stream", bufs=3))
+        stream = ctx.enter_context(tc.tile_pool(name="stream", bufs=4))
         score_banks = ctx.enter_context(tc.psum_pool(name="score_banks", bufs=SCORE_BANKS))
         ring_banks = ctx.enter_context(tc.psum_pool(name="ring_banks", bufs=RING_BANKS))
 
@@ -170,8 +169,10 @@ def tile_nsa_pa_t_kernel(tc, queries, comp_k, values, gate_cmp, out):
         def copy_out(i):
             grouped = stream.tile([P, PASSES, P, PACK], BF16, align_bytes=64)
             words = flipped_of[i][:].rearrange("p (g j) t -> p g t j", j=PACK)
-            nc.scalar.copy(out=grouped[:, :, 0:SCALAR_COLS, :], in_=words[:, :, 0:SCALAR_COLS, :])
-            nc.vector.tensor_copy(out=grouped[:, :, SCALAR_COLS:P, :], in_=words[:, :, SCALAR_COLS:P, :])
+            if i % GROUP == 0:
+                nc.vector.tensor_copy(out=grouped[:], in_=words)
+            else:
+                nc.scalar.copy(out=grouped[:], in_=words)
             grouped_of[i] = grouped
 
         def quantise(i):

@@ -68,6 +68,8 @@ def tile_nsa_pa_t_kernel(tc, queries, comp_k, values, gate_cmp, out):
 
         identity = keep.tile([P, P], BF16)
         make_identity(nc, identity[:])
+        identity_f32 = keep.tile([P, P], F32)
+        make_identity(nc, identity_f32[:])
         warm = keep.tile([P, 1], F32)
         nc.vector.memset(warm[:], 0.0)
         nc.scalar.activation(out=warm[:], in_=warm[:], func=EXP)
@@ -78,7 +80,8 @@ def tile_nsa_pa_t_kernel(tc, queries, comp_k, values, gate_cmp, out):
             for j in range(PACK):
                 nc.tensor.transpose(kT_ps[:, j, :], k_sb[:, g, j, :], identity[:])
             nc.vector.tensor_copy(
-                out=kT_sb[:, g * K_PASS : (g + 1) * K_PASS], in_=kT_ps[:].rearrange("p j n -> p (j n)")
+                out=kT_sb[:, g * K_PASS : (g + 1) * K_PASS].rearrange("d (u p h) -> d u p h", u=2, h=2),
+                in_=kT_ps[:].rearrange("d (u h) p -> d u p h", u=2),
             )
 
         block_sums = keep.tile([P, PASSES, PACK, D], F32)
@@ -161,18 +164,16 @@ def tile_nsa_pa_t_kernel(tc, queries, comp_k, values, gate_cmp, out):
 
         def transpose_e(i, g):
             if g == 0:
-                flipped = ring_banks.tile([P, PASSES * PACK, P], BF16, tag="ring")
+                flipped = ring_banks.tile([P, PASSES * 2, P], F32, tag="ring")
                 flipped_of[i] = flipped
-            for a in range(g * PACK, (g + 1) * PACK):
-                nc.tensor.transpose(flipped_of[i][:, a, :], e_of[i][:, a * P : (a + 1) * P], identity[:])
+            words = e_of[i][:].bitcast(F32)
+            for a in range(g * 2, (g + 1) * 2):
+                nc.tensor.transpose(flipped_of[i][:, a, :], words[:, a * P : (a + 1) * P], identity_f32[:])
 
         def copy_out(i):
             grouped = stream.tile([P, PASSES, P, PACK], BF16, align_bytes=64)
-            words = flipped_of[i][:].rearrange("p (g j) t -> p g t j", j=PACK)
-            if i % GROUP == 0:
-                nc.vector.tensor_copy(out=grouped[:], in_=words)
-            else:
-                nc.scalar.copy(out=grouped[:], in_=words)
+            halves = flipped_of[i][:].rearrange("p (g u) t -> p g t u", u=2)
+            nc.scalar.copy(out=grouped[:].bitcast(F32), in_=halves)
             grouped_of[i] = grouped
 
         def quantise(i):

@@ -35,7 +35,13 @@ COPY_BEHIND = 1
 QUANTISE_BEHIND = 2
 Q_TRANSPOSE_AHEAD = 5
 Q_COPY_AHEAD = 4
-MX_LAG = 1
+V_CHUNKS = 16
+V_ROWS = 4
+BLOCKS_A_CHUNK = N // V_CHUNKS
+CHUNKS_A_PASS = V_CHUNKS // PASSES
+V_FIRST_STEP = 1
+V_FIRST_MX = V_FIRST_STEP + V_CHUNKS // 2 + 2
+V_TILE = TILES
 
 FLOPS = 2 * 2 * T * N * D
 
@@ -47,7 +53,6 @@ def tile_nsa_pa_t_kernel(tc, queries, comp_k, values, gate_cmp, out):
 
     with ExitStack() as ctx:
         keep = ctx.enter_context(tc.tile_pool(name="keep", bufs=1))
-        pooling = ctx.enter_context(tc.tile_pool(name="pooling", bufs=1))
         small = ctx.enter_context(tc.tile_pool(name="small", bufs=4))
         stream = ctx.enter_context(tc.tile_pool(name="stream", bufs=4))
         score_banks = ctx.enter_context(tc.psum_pool(name="score_banks", bufs=SCORE_BANKS))
@@ -59,10 +64,11 @@ def tile_nsa_pa_t_kernel(tc, queries, comp_k, values, gate_cmp, out):
         nc.sync.dma_start(out=q_sb[:, 0:Q_LOAD, :], in_=q_view[:, 0:Q_LOAD, :])
         gate_sb = keep.tile([P, TILES], BF16)
         nc.sync.dma_start(out=gate_sb[:], in_=gate_cmp[0].rearrange("(p c) -> p c", c=TILES))
-        v_sb = keep.tile([P, PASSES, PACK * BS, D], BF16)
-        v_view = values[0].rearrange("(g p r) d -> p g r d", g=PASSES, r=PACK * BS)
+        v_sb = keep.tile([P, V_CHUNKS, V_ROWS, D], BF16)
+        v_view = values[0].rearrange("(s r x) d -> r s x d", s=V_CHUNKS, x=V_ROWS)
         for g in range(PASSES):
-            nc.sync.dma_start(out=v_sb[:, g], in_=v_view[:, g])
+            chunks = slice(g * CHUNKS_A_PASS, (g + 1) * CHUNKS_A_PASS)
+            nc.sync.dma_start(out=v_sb[:, chunks], in_=v_view[:, chunks])
         for first in range(Q_LOAD, TILES, Q_LOAD):
             nc.sync.dma_start(out=q_sb[:, first : first + Q_LOAD, :], in_=q_view[:, first : first + Q_LOAD, :])
 
@@ -84,16 +90,11 @@ def tile_nsa_pa_t_kernel(tc, queries, comp_k, values, gate_cmp, out):
                 in_=kT_ps[:].rearrange("d (u h) p -> d u p h", u=2),
             )
 
-        block_sums = keep.tile([P, PASSES, PACK, D], F32)
-        for g in range(PASSES):
-            rows8 = v_sb[:, g].rearrange("p (j i) d -> p j (i d)", i=BS)
-            rows4 = pooling.tile([P, PACK, 4 * D], F32)
-            nc.gpsimd.tensor_tensor(out=rows4[:], in0=rows8[:, :, 0 : 4 * D], in1=rows8[:, :, 4 * D : 8 * D], op=ALU.add)
-            rows2 = pooling.tile([P, PACK, 2 * D], F32)
-            nc.gpsimd.tensor_tensor(out=rows2[:], in0=rows4[:, :, 0 : 2 * D], in1=rows4[:, :, 2 * D : 4 * D], op=ALU.add)
-            nc.gpsimd.tensor_tensor(out=block_sums[:, g], in0=rows2[:, :, 0:D], in1=rows2[:, :, D : 2 * D], op=ALU.add)
-        v_codes = keep.tile([P, PASSES, D], U32, align_bytes=64)
-        v_scales = keep.tile([P, PASSES, D], U8, align_bytes=64)
+        pair_sum = keep.tile([P, BLOCKS_A_CHUNK], BF16)
+        column_pairs = identity[:].rearrange("r (c two) -> r c two", two=2)
+        nc.vector.tensor_tensor(out=pair_sum[:], in0=column_pairs[:, :, 0], in1=column_pairs[:, :, 1], op=ALU.add)
+        v_codes = keep.tile([P, PASSES * D], U32, align_bytes=64)
+        v_scales = keep.tile([P, PASSES * D], U8, align_bytes=64)
 
         e_codes = keep.tile([P, TILES, PASSES * P], U32, align_bytes=64)
         e_scales = keep.tile([P, TILES, PASSES * P], U8, align_bytes=64)
@@ -106,6 +107,7 @@ def tile_nsa_pa_t_kernel(tc, queries, comp_k, values, gate_cmp, out):
         flipped_of = {}
         grouped_of = {}
         out_of = {}
+        v_sums_of = {}
 
         def exists(tile_index):
             return 0 <= tile_index < TILES
@@ -162,6 +164,32 @@ def tile_nsa_pa_t_kernel(tc, queries, comp_k, values, gate_cmp, out):
                 accum_out=row_sums[:, i, g : g + 1],
             )
 
+        def sum_blocks(s):
+            g, place = divmod(s, CHUNKS_A_PASS)
+            if place == 0:
+                v_sums = ring_banks.tile([P, K_PASS], F32, tag="ring")
+                v_sums_of[g] = v_sums
+            for x in range(V_ROWS):
+                nc.tensor.matmul(
+                    out=v_sums_of[g][:, place * BLOCKS_A_CHUNK : (place + 1) * BLOCKS_A_CHUNK],
+                    lhsT=v_sb[:, s, x, :],
+                    rhs=pair_sum[:],
+                    start=(x == 0),
+                    stop=(x == V_ROWS - 1),
+                )
+
+        def round_means(g):
+            if g == 0:
+                means = stream.tile([P, N], BF16, tag="e")
+                e_of[V_TILE] = means
+            nc.vector.tensor_scalar(
+                out=e_of[V_TILE][:, g * K_PASS : (g + 1) * K_PASS].rearrange("d (u p h) -> d u p h", u=2, h=2),
+                in0=v_sums_of[g][:].rearrange("d (p u h) -> d u p h", u=2, h=2),
+                scalar1=1.0 / BS,
+                scalar2=None,
+                op0=ALU.mult,
+            )
+
         def transpose_e(i, g):
             if g == 0:
                 flipped = ring_banks.tile([P, PASSES * 2, P], F32, tag="ring")
@@ -177,9 +205,10 @@ def tile_nsa_pa_t_kernel(tc, queries, comp_k, values, gate_cmp, out):
             grouped_of[i] = grouped
 
         def quantise(i):
+            codes, scale_bytes = (v_codes[:], v_scales[:]) if i == V_TILE else (e_codes[:, i, :], e_scales[:, i, :])
             nc.vector.quantize_mx(
-                out=e_codes[:, i, :].bitcast(FP8X4),
-                scales=e_scales[:, i, :],
+                out=codes.bitcast(FP8X4),
+                scales=scale_bytes,
                 in_=grouped_of[i][:].rearrange("p g t j -> p (g t j)"),
             )
 
@@ -192,8 +221,8 @@ def tile_nsa_pa_t_kernel(tc, queries, comp_k, values, gate_cmp, out):
                         out=out_ps[:, c, :],
                         lhsT=e_codes[:, i, g * P : (g + 1) * P].bitcast(FP8X4),
                         lhsT_scale=e_scales[:, i, g * P : (g + 1) * P],
-                        rhs=v_codes[:, g, :].bitcast(FP8X4),
-                        rhs_scale=v_scales[:, g, :],
+                        rhs=v_codes[:, g * D : (g + 1) * D].bitcast(FP8X4),
+                        rhs_scale=v_scales[:, g * D : (g + 1) * D],
                         start=(g == 0),
                         stop=(g == PASSES - 1),
                     )
@@ -214,26 +243,11 @@ def tile_nsa_pa_t_kernel(tc, queries, comp_k, values, gate_cmp, out):
             )
             nc.sync.dma_start(out=out_view[:, tiles, :], in_=out_sb[:])
 
-        mx_offset = GROUP + QUANTISE_BEHIND + GROUP * MX_LAG
-        for step in range(-Q_TRANSPOSE_AHEAD, GROUP * (GROUPS - 1) + mx_offset + 1):
-            mx_group, mx_rest = divmod(step - mx_offset, GROUP)
-            mx_due = mx_rest == 0 and 0 <= mx_group < GROUPS
-            if mx_due and mx_group == 0:
-                v_grouped = stream.tile([P, PASSES, D, PACK], BF16, align_bytes=64, tag="grouped")
-                for g in range(PASSES):
-                    nc.gpsimd.tensor_scalar(
-                        out=v_grouped[:, g],
-                        in0=block_sums[:, g].rearrange("p j d -> p d j"),
-                        scalar1=1.0 / BS,
-                        scalar2=0.0,
-                        op0=ALU.mult,
-                        op1=ALU.add,
-                    )
-                nc.vector.quantize_mx(
-                    out=v_codes[:].rearrange("p g d -> p (g d)").bitcast(FP8X4),
-                    scales=v_scales[:].rearrange("p g d -> p (g d)"),
-                    in_=v_grouped[:].rearrange("p g d j -> p (g d j)"),
-                )
+        mx_groups_of = {}
+        for k in range(GROUPS):
+            mx_step = max(GROUP * k + GROUP + QUANTISE_BEHIND, V_FIRST_MX + 2 * k)
+            mx_groups_of.setdefault(mx_step, []).append(k)
+        for step in range(-Q_TRANSPOSE_AHEAD, max(mx_groups_of) + 1):
             if exists(step + MAX_AHEAD):
                 row_maximum(step + MAX_AHEAD)
             for g in range(PASSES):
@@ -245,10 +259,21 @@ def tile_nsa_pa_t_kernel(tc, queries, comp_k, values, gate_cmp, out):
                 copy_out(step - COPY_BEHIND)
             if exists(step - QUANTISE_BEHIND):
                 quantise(step - QUANTISE_BEHIND)
+            for s in range(2 * (step - V_FIRST_STEP), 2 * (step - V_FIRST_STEP) + 2):
+                if 0 <= s < V_CHUNKS:
+                    sum_blocks(s)
+                    if (s + 1) % CHUNKS_A_PASS == 0:
+                        round_means(s // CHUNKS_A_PASS)
+            if step == V_FIRST_STEP + V_CHUNKS // 2:
+                for g in range(PASSES):
+                    transpose_e(V_TILE, g)
+                copy_out(V_TILE)
+            if step == V_FIRST_STEP + V_CHUNKS // 2 + 1:
+                quantise(V_TILE)
             if exists(step + Q_COPY_AHEAD) and (step + Q_COPY_AHEAD) % GROUP == 0:
                 copy_queries((step + Q_COPY_AHEAD) // GROUP)
             if exists(step + Q_TRANSPOSE_AHEAD) and (step + Q_TRANSPOSE_AHEAD) % GROUP == 0:
                 transpose_queries((step + Q_TRANSPOSE_AHEAD) // GROUP)
-            if mx_due:
-                weighted_sums(mx_group)
-                finish(mx_group)
+            for k in mx_groups_of.get(step, []):
+                weighted_sums(k)
+                finish(k)

@@ -40,7 +40,7 @@ V_ROWS = 4
 BLOCKS_A_CHUNK = N // V_CHUNKS
 CHUNKS_A_PASS = V_CHUNKS // PASSES
 V_FIRST_STEP = 1
-V_FIRST_MX = V_FIRST_STEP + V_CHUNKS // 2 + 2
+V_FIRST_MX = V_FIRST_STEP + V_CHUNKS // 2 + 1
 V_TILE = TILES
 
 FLOPS = 2 * 2 * T * N * D
@@ -59,9 +59,12 @@ def tile_nsa_pa_t_kernel(tc, queries, comp_k, values, gate_cmp, out):
         ring_banks = ctx.enter_context(tc.psum_pool(name="ring_banks", bufs=RING_BANKS))
 
         k_sb = keep.tile([P, PASSES, PACK, D], BF16)
-        nc.sync.dma_start(out=k_sb[:], in_=comp_k[0].rearrange("(g p j) d -> p g j d", g=PASSES, j=PACK))
+        k_view = comp_k[0].rearrange("(g p j) d -> p g j d", g=PASSES, j=PACK)
         q_sb = keep.tile([P, TILES, D], BF16)
-        nc.sync.dma_start(out=q_sb[:, 0:Q_LOAD, :], in_=q_view[:, 0:Q_LOAD, :])
+        nc.sync.dma_start(out=k_sb[:, 0], in_=k_view[:, 0])
+        nc.sync.dma_start(out=q_sb[:, 0:GROUP, :], in_=q_view[:, 0:GROUP, :])
+        nc.sync.dma_start(out=k_sb[:, 1], in_=k_view[:, 1])
+        nc.sync.dma_start(out=q_sb[:, GROUP:Q_LOAD, :], in_=q_view[:, GROUP:Q_LOAD, :])
         gate_sb = keep.tile([P, TILES], BF16)
         nc.sync.dma_start(out=gate_sb[:], in_=gate_cmp[0].rearrange("(p c) -> p c", c=TILES))
         v_sb = keep.tile([P, V_CHUNKS, V_ROWS, D], BF16)
@@ -81,11 +84,12 @@ def tile_nsa_pa_t_kernel(tc, queries, comp_k, values, gate_cmp, out):
         nc.scalar.activation(out=warm[:], in_=warm[:], func=EXP)
 
         kT_sb = keep.tile([P, N], BF16)
-        for g in range(PASSES):
+
+        def transpose_keys(g, copy):
             kT_ps = ring_banks.tile([P, PACK, P], BF16, tag="ring")
             for j in range(PACK):
                 nc.tensor.transpose(kT_ps[:, j, :], k_sb[:, g, j, :], identity[:])
-            nc.vector.tensor_copy(
+            copy(
                 out=kT_sb[:, g * K_PASS : (g + 1) * K_PASS].rearrange("d (u p h) -> d u p h", u=2, h=2),
                 in_=kT_ps[:].rearrange("d (u h) p -> d u p h", u=2),
             )
@@ -107,6 +111,7 @@ def tile_nsa_pa_t_kernel(tc, queries, comp_k, values, gate_cmp, out):
         flipped_of = {}
         grouped_of = {}
         out_of = {}
+        factor_of = {}
         v_sums_of = {}
 
         def exists(tile_index):
@@ -120,7 +125,10 @@ def tile_nsa_pa_t_kernel(tc, queries, comp_k, values, gate_cmp, out):
 
         def copy_queries(group):
             qT = stream.tile([P, GROUP, P], BF16)
-            nc.vector.tensor_copy(out=qT[:], in_=qT_ps_of[group][:])
+            if group == 0:
+                nc.scalar.copy(out=qT[:], in_=qT_ps_of[group][:])
+            else:
+                nc.vector.tensor_copy(out=qT[:], in_=qT_ps_of[group][:])
             qT_of[group] = qT
 
         def scores(bank_number):
@@ -201,7 +209,10 @@ def tile_nsa_pa_t_kernel(tc, queries, comp_k, values, gate_cmp, out):
         def copy_out(i):
             grouped = stream.tile([P, PASSES, P, PACK], BF16, align_bytes=64)
             halves = flipped_of[i][:].rearrange("p (g u) t -> p g t u", u=2)
-            nc.scalar.copy(out=grouped[:].bitcast(F32), in_=halves)
+            if TILES - 3 <= i <= TILES - 2:
+                nc.vector.tensor_copy(out=grouped[:].bitcast(F32), in_=halves)
+            else:
+                nc.scalar.copy(out=grouped[:].bitcast(F32), in_=halves)
             grouped_of[i] = grouped
 
         def quantise(i):
@@ -212,10 +223,10 @@ def tile_nsa_pa_t_kernel(tc, queries, comp_k, values, gate_cmp, out):
                 in_=grouped_of[i][:].rearrange("p g t j -> p (g t j)"),
             )
 
-        def weighted_sums(group):
+        def weighted_sums(first, count):
             out_ps = ring_banks.tile([P, GROUP, D], F32, tag="ring")
-            for c in range(GROUP):
-                i = group * GROUP + c
+            for c in range(count):
+                i = first + c
                 for g in range(PASSES):
                     nc.tensor.matmul_mx(
                         out=out_ps[:, c, :],
@@ -226,39 +237,57 @@ def tile_nsa_pa_t_kernel(tc, queries, comp_k, values, gate_cmp, out):
                         start=(g == 0),
                         stop=(g == PASSES - 1),
                     )
-            out_of[group] = out_ps
+            out_of[first] = out_ps
 
-        def finish(group):
-            tiles = slice(group * GROUP, (group + 1) * GROUP)
+        def factors(first, count):
+            tiles = slice(first, first + count)
             factor = small.tile([P, GROUP], F32)
-            nc.vector.tensor_reduce(out=factor[:], in_=row_sums[:, tiles, :], axis=X_AXIS, op=ALU.add)
-            nc.vector.reciprocal(out=factor[:], in_=factor[:])
-            nc.vector.tensor_tensor(out=factor[:], in0=factor[:], in1=gate_sb[:, tiles], op=ALU.mult)
+            nc.vector.tensor_reduce(out=factor[:, 0:count], in_=row_sums[:, tiles, :], axis=X_AXIS, op=ALU.add)
+            nc.vector.reciprocal(out=factor[:, 0:count], in_=factor[:, 0:count])
+            nc.vector.tensor_tensor(out=factor[:, 0:count], in0=factor[:, 0:count], in1=gate_sb[:, tiles], op=ALU.mult)
+            factor_of[first] = factor
+
+        def scale_and_store(first, count):
             out_sb = stream.tile([P, GROUP, D], F32)
             nc.vector.tensor_tensor(
-                out=out_sb[:],
-                in0=out_of[group][:],
-                in1=factor[:].unsqueeze(2).to_broadcast([P, GROUP, D]),
+                out=out_sb[:, 0:count, :],
+                in0=out_of[first][:, 0:count, :],
+                in1=factor_of[first][:, 0:count].unsqueeze(2).to_broadcast([P, count, D]),
                 op=ALU.mult,
             )
-            nc.sync.dma_start(out=out_view[:, tiles, :], in_=out_sb[:])
+            nc.sync.dma_start(out=out_view[:, first : first + count, :], in_=out_sb[:, 0:count, :])
 
-        mx_groups_of = {}
-        for k in range(GROUPS):
-            mx_step = max(GROUP * k + GROUP + QUANTISE_BEHIND, V_FIRST_MX + 2 * k)
-            mx_groups_of.setdefault(mx_step, []).append(k)
-        for step in range(-Q_TRANSPOSE_AHEAD, max(mx_groups_of) + 1):
+        runs = [(first, GROUP) for first in range(0, TILES - GROUP, GROUP)]
+        runs.extend([(TILES - GROUP, GROUP - 1), (TILES - 1, 1)])
+        factors_in = {}
+        passes_in = {}
+        stores_in = {}
+        for number, (first, count) in enumerate(runs):
+            last = first + count - 1
+            mx_step = max(last + QUANTISE_BEHIND, V_FIRST_MX + 2 * number)
+            factors_in.setdefault(last + 1, []).append((first, count))
+            passes_in.setdefault(mx_step, []).append((first, count))
+            stores_in.setdefault(mx_step + 1, []).append((first, count))
+        transpose_keys(0, nc.vector.tensor_copy)
+        transpose_queries(0)
+        copy_queries(0)
+        transpose_keys(1, nc.scalar.copy)
+        for step in range(-Q_COPY_AHEAD + 1, max(stores_in) + 1):
             if exists(step + MAX_AHEAD):
                 row_maximum(step + MAX_AHEAD)
+            for first, count in stores_in.get(step, []):
+                scale_and_store(first, count)
             for g in range(PASSES):
                 if exists(step):
                     exponential(step, g)
                     transpose_e(step, g)
                 scores(PASSES * step + g + SCORE_BANKS)
-            if exists(step - COPY_BEHIND):
-                copy_out(step - COPY_BEHIND)
             if exists(step - QUANTISE_BEHIND):
                 quantise(step - QUANTISE_BEHIND)
+            for first, count in factors_in.get(step, []):
+                factors(first, count)
+            if exists(step - COPY_BEHIND):
+                copy_out(step - COPY_BEHIND)
             for s in range(2 * (step - V_FIRST_STEP), 2 * (step - V_FIRST_STEP) + 2):
                 if 0 <= s < V_CHUNKS:
                     sum_blocks(s)
@@ -274,6 +303,5 @@ def tile_nsa_pa_t_kernel(tc, queries, comp_k, values, gate_cmp, out):
                 copy_queries((step + Q_COPY_AHEAD) // GROUP)
             if exists(step + Q_TRANSPOSE_AHEAD) and (step + Q_TRANSPOSE_AHEAD) % GROUP == 0:
                 transpose_queries((step + Q_TRANSPOSE_AHEAD) // GROUP)
-            for k in mx_groups_of.get(step, []):
-                weighted_sums(k)
-                finish(k)
+            for first, count in passes_in.get(step, []):
+                weighted_sums(first, count)

@@ -62,8 +62,9 @@ def tile_nsa_pa_t_kernel(tc, queries, comp_k, values, gate_cmp, out):
         k_view = comp_k[0].rearrange("(g p j) d -> p g j d", g=PASSES, j=PACK)
         q_sb = keep.tile([P, TILES, D], BF16)
         nc.sync.dma_start(out=k_sb[:, 0], in_=k_view[:, 0])
-        nc.sync.dma_start(out=q_sb[:, 0:GROUP, :], in_=q_view[:, 0:GROUP, :])
+        nc.sync.dma_start(out=q_sb[:, 0:1, :], in_=q_view[:, 0:1, :])
         nc.sync.dma_start(out=k_sb[:, 1], in_=k_view[:, 1])
+        nc.sync.dma_start(out=q_sb[:, 1:GROUP, :], in_=q_view[:, 1:GROUP, :])
         nc.sync.dma_start(out=q_sb[:, GROUP:Q_LOAD, :], in_=q_view[:, GROUP:Q_LOAD, :])
         gate_sb = keep.tile([P, TILES], BF16)
         nc.sync.dma_start(out=gate_sb[:], in_=gate_cmp[0].rearrange("(p c) -> p c", c=TILES))
@@ -117,23 +118,25 @@ def tile_nsa_pa_t_kernel(tc, queries, comp_k, values, gate_cmp, out):
         def exists(tile_index):
             return 0 <= tile_index < TILES
 
-        def transpose_queries(group):
+        def transpose_queries(group, first=0, count=GROUP):
             qT_ps = ring_banks.tile([P, GROUP, P], BF16, tag="ring")
-            for c in range(GROUP):
+            for c in range(first, first + count):
                 nc.tensor.transpose(qT_ps[:, c, :], q_sb[:, group * GROUP + c, :], identity[:])
             qT_ps_of[group] = qT_ps
 
-        def copy_queries(group):
-            qT = stream.tile([P, GROUP, P], BF16)
+        def copy_queries(group, first=0, count=GROUP):
+            if first == 0:
+                qT = stream.tile([P, GROUP, P], BF16)
+                qT_of[group] = qT
+            part = slice(first, first + count)
             if group == 0:
-                nc.scalar.copy(out=qT[:], in_=qT_ps_of[group][:])
+                nc.scalar.copy(out=qT_of[group][:, part, :], in_=qT_ps_of[group][:, part, :])
             else:
-                nc.vector.tensor_copy(out=qT[:], in_=qT_ps_of[group][:])
-            qT_of[group] = qT
+                nc.vector.tensor_copy(out=qT_of[group][:, part, :], in_=qT_ps_of[group][:, part, :])
 
         def scores(bank_number):
             i, g = divmod(bank_number, PASSES)
-            if exists(i):
+            if exists(i) and (i, g) not in scores_of:
                 bank = score_banks.tile([P, K_PASS], F32)
                 nc.tensor.matmul(
                     out=bank[:],
@@ -198,13 +201,34 @@ def tile_nsa_pa_t_kernel(tc, queries, comp_k, values, gate_cmp, out):
                 op0=ALU.mult,
             )
 
+        def in_halves(i):
+            return i == TILES - 1
+
         def transpose_e(i, g):
-            if g == 0:
+            if g == 0 or in_halves(i):
                 flipped = ring_banks.tile([P, PASSES * 2, P], F32, tag="ring")
-                flipped_of[i] = flipped
+                flipped_of[(i, g) if in_halves(i) else i] = flipped
+            bank = flipped_of[(i, g) if in_halves(i) else i]
             words = e_of[i][:].bitcast(F32)
             for a in range(g * 2, (g + 1) * 2):
-                nc.tensor.transpose(flipped_of[i][:, a, :], words[:, a * P : (a + 1) * P], identity_f32[:])
+                nc.tensor.transpose(bank[:, a, :], words[:, a * P : (a + 1) * P], identity_f32[:])
+
+        def copy_out_half(i, g):
+            if g == 0:
+                grouped = stream.tile([P, PASSES, P, PACK], BF16, align_bytes=64)
+                grouped_of[i] = grouped
+            halves = flipped_of[(i, g)][:, g * 2 : (g + 1) * 2, :].rearrange("p u t -> p t u")
+            if g == 0:
+                nc.vector.tensor_copy(out=grouped_of[i][:, g].bitcast(F32), in_=halves)
+            else:
+                nc.scalar.copy(out=grouped_of[i][:, g].bitcast(F32), in_=halves)
+
+        def quantise_half(i, g):
+            nc.vector.quantize_mx(
+                out=e_codes[:, i, g * P : (g + 1) * P].bitcast(FP8X4),
+                scales=e_scales[:, i, g * P : (g + 1) * P],
+                in_=grouped_of[i][:, g].rearrange("p t j -> p (t j)"),
+            )
 
         def copy_out(i):
             grouped = stream.tile([P, PASSES, P, PACK], BF16, align_bytes=64)
@@ -269,9 +293,13 @@ def tile_nsa_pa_t_kernel(tc, queries, comp_k, values, gate_cmp, out):
             passes_in.setdefault(mx_step, []).append((first, count))
             stores_in.setdefault(mx_step + 1, []).append((first, count))
         transpose_keys(0, nc.vector.tensor_copy)
-        transpose_queries(0)
-        copy_queries(0)
+        transpose_queries(0, 0, 1)
+        copy_queries(0, 0, 1)
         transpose_keys(1, nc.scalar.copy)
+        scores(0)
+        transpose_queries(0, 1, GROUP - 1)
+        copy_queries(0, 1, GROUP - 1)
+        scores(1)
         for step in range(-Q_COPY_AHEAD + 1, max(stores_in) + 1):
             if exists(step + MAX_AHEAD):
                 row_maximum(step + MAX_AHEAD)
@@ -282,12 +310,20 @@ def tile_nsa_pa_t_kernel(tc, queries, comp_k, values, gate_cmp, out):
                     exponential(step, g)
                     transpose_e(step, g)
                 scores(PASSES * step + g + SCORE_BANKS)
-            if exists(step - QUANTISE_BEHIND):
+            if in_halves(step - QUANTISE_BEHIND):
+                quantise_half(step - QUANTISE_BEHIND, 1)
+            elif exists(step - QUANTISE_BEHIND):
                 quantise(step - QUANTISE_BEHIND)
+            if in_halves(step - COPY_BEHIND):
+                quantise_half(step - COPY_BEHIND, 0)
             for first, count in factors_in.get(step, []):
                 factors(first, count)
-            if exists(step - COPY_BEHIND):
+            if in_halves(step - COPY_BEHIND):
+                copy_out_half(step - COPY_BEHIND, 1)
+            elif exists(step - COPY_BEHIND):
                 copy_out(step - COPY_BEHIND)
+            if in_halves(step):
+                copy_out_half(step, 0)
             for s in range(2 * (step - V_FIRST_STEP), 2 * (step - V_FIRST_STEP) + 2):
                 if 0 <= s < V_CHUNKS:
                     sum_blocks(s)

@@ -27,8 +27,8 @@ Q_LOAD = 8
 SCALE = D ** -0.5
 
 
-SCORE_BANKS = 5
-RING_BANKS = 3
+SCORE_BANKS = 6
+PSUM_BANKS = 8
 
 MAX_AHEAD = 1
 COPY_BEHIND = 1
@@ -55,8 +55,7 @@ def tile_nsa_pa_t_kernel(tc, queries, comp_k, values, gate_cmp, out):
         keep = ctx.enter_context(tc.tile_pool(name="keep", bufs=1))
         small = ctx.enter_context(tc.tile_pool(name="small", bufs=4))
         stream = ctx.enter_context(tc.tile_pool(name="stream", bufs=4))
-        score_banks = ctx.enter_context(tc.psum_pool(name="score_banks", bufs=SCORE_BANKS))
-        ring_banks = ctx.enter_context(tc.psum_pool(name="ring_banks", bufs=RING_BANKS))
+        ring_banks = ctx.enter_context(tc.psum_pool(name="ring_banks", bufs=PSUM_BANKS))
 
         k_sb = keep.tile([P, PASSES, PACK, D], BF16)
         k_view = comp_k[0].rearrange("(g p j) d -> p g j d", g=PASSES, j=PACK)
@@ -137,7 +136,7 @@ def tile_nsa_pa_t_kernel(tc, queries, comp_k, values, gate_cmp, out):
         def scores(bank_number):
             i, g = divmod(bank_number, PASSES)
             if exists(i) and (i, g) not in scores_of:
-                bank = score_banks.tile([P, K_PASS], F32)
+                bank = ring_banks.tile([P, K_PASS], F32, tag="ring")
                 nc.tensor.matmul(
                     out=bank[:],
                     lhsT=qT_of[i // GROUP][:, i % GROUP, :],

@@ -24,6 +24,7 @@ TILES = T // P
 GROUP = 4
 GROUPS = TILES // GROUP
 Q_LOAD = 8
+FACTOR_BATCH = 2 * GROUP
 SCALE = D ** -0.5
 
 
@@ -200,6 +201,11 @@ def tile_nsa_pa_t_kernel(tc, queries, comp_k, values, gate_cmp, out):
                 op0=ALU.mult,
             )
 
+        pair_of = {}
+
+        def in_pair(i):
+            return i < TILES - GROUP
+
         def in_halves(i):
             return i == TILES - 1
 
@@ -230,20 +236,31 @@ def tile_nsa_pa_t_kernel(tc, queries, comp_k, values, gate_cmp, out):
             )
 
         def copy_out(i):
-            grouped = stream.tile([P, PASSES, P, PACK], BF16, align_bytes=64)
-            halves = flipped_of[i][:].rearrange("p (g u) t -> p g t u", u=2)
-            if TILES - 3 <= i <= TILES - 2:
-                nc.vector.tensor_copy(out=grouped[:].bitcast(F32), in_=halves)
+            if i % 2 == 0 or not in_pair(i):
+                grouped = stream.tile([P, 2, PASSES, P, PACK], BF16, align_bytes=64)
+                place = 0
             else:
-                nc.scalar.copy(out=grouped[:].bitcast(F32), in_=halves)
-            grouped_of[i] = grouped
+                grouped = pair_of[i - 1]
+                place = 1
+            pair_of[i] = grouped
+            halves = flipped_of[i][:].rearrange("p (g u) t -> p g t u", u=2)
+            if TILES - 3 <= i <= TILES - 2 or (i % 16 == 11 and in_pair(i)):
+                nc.vector.tensor_copy(out=grouped[:, place].bitcast(F32), in_=halves)
+            else:
+                nc.scalar.copy(out=grouped[:, place].bitcast(F32), in_=halves)
 
         def quantise(i):
-            codes, scale_bytes = (v_codes[:], v_scales[:]) if i == V_TILE else (e_codes[:, i, :], e_scales[:, i, :])
+            if in_pair(i) and i % 2 == 0:
+                return
+            count = 2 if in_pair(i) else 1
+            tiles = slice(i + 1 - count, i + 1)
+            codes, scale_bytes = (v_codes[:], v_scales[:]) if i == V_TILE else (e_codes[:, tiles, :], e_scales[:, tiles, :])
+            if i != V_TILE:
+                codes, scale_bytes = codes.rearrange("p c w -> p (c w)"), scale_bytes.rearrange("p c w -> p (c w)")
             nc.vector.quantize_mx(
                 out=codes.bitcast(FP8X4),
                 scales=scale_bytes,
-                in_=grouped_of[i][:].rearrange("p g t j -> p (g t j)"),
+                in_=pair_of[i][:, 0:count].rearrange("p c g t j -> p (c g t j)"),
             )
 
         def weighted_sums(first, count):
@@ -264,11 +281,12 @@ def tile_nsa_pa_t_kernel(tc, queries, comp_k, values, gate_cmp, out):
 
         def factors(first, count):
             tiles = slice(first, first + count)
-            factor = small.tile([P, GROUP], F32)
+            factor = small.tile([P, FACTOR_BATCH], F32)
             nc.vector.tensor_reduce(out=factor[:, 0:count], in_=row_sums[:, tiles, :], axis=X_AXIS, op=ALU.add)
             nc.vector.reciprocal(out=factor[:, 0:count], in_=factor[:, 0:count])
             nc.vector.tensor_tensor(out=factor[:, 0:count], in0=factor[:, 0:count], in1=gate_sb[:, tiles], op=ALU.mult)
-            factor_of[first] = factor
+            for group_first in range(first, first + count, GROUP):
+                factor_of[group_first] = factor[:, group_first - first : group_first - first + GROUP]
 
         def scale_and_store(first, count):
             out_sb = stream.tile([P, GROUP, D], F32)
@@ -282,13 +300,20 @@ def tile_nsa_pa_t_kernel(tc, queries, comp_k, values, gate_cmp, out):
 
         runs = [(first, GROUP) for first in range(0, TILES - GROUP, GROUP)]
         runs.extend([(TILES - GROUP, GROUP - 1), (TILES - 1, 1)])
+        BATCHED_TILES = TILES - FACTOR_BATCH
         factors_in = {}
         passes_in = {}
         stores_in = {}
         for number, (first, count) in enumerate(runs):
             last = first + count - 1
-            mx_step = max(last + QUANTISE_BEHIND, V_FIRST_MX + 2 * number)
-            factors_in.setdefault(last + 1, []).append((first, count))
+            if last < BATCHED_TILES:
+                if first % FACTOR_BATCH == 0:
+                    factors_in.setdefault(first + FACTOR_BATCH, []).append((first, FACTOR_BATCH))
+                behind = GROUP if last == BATCHED_TILES - 1 else GROUP + 2
+            else:
+                factors_in.setdefault(last + 1, []).append((first, count))
+                behind = QUANTISE_BEHIND
+            mx_step = max(last + behind, V_FIRST_MX + 2 * number)
             passes_in.setdefault(mx_step, []).append((first, count))
             stores_in.setdefault(mx_step + 1, []).append((first, count))
         transpose_keys(0, nc.vector.tensor_copy)

@@ -42,6 +42,7 @@ BLOCKS_A_CHUNK = N // V_CHUNKS
 CHUNKS_A_PASS = V_CHUNKS // PASSES
 V_FIRST_STEP = 1
 V_FIRST_MX = V_FIRST_STEP + V_CHUNKS // 2 + 1
+WARM_UP = 4
 V_TILE = TILES
 
 FLOPS = 2 * 2 * T * N * D
@@ -83,6 +84,12 @@ def tile_nsa_pa_t_kernel(tc, queries, comp_k, values, gate_cmp, out):
         warm = keep.tile([P, 1], F32)
         nc.vector.memset(warm[:], 0.0)
         nc.scalar.activation(out=warm[:], in_=warm[:], func=EXP)
+
+        zeros = keep.tile([P, K_PASS], BF16)
+        nc.vector.memset(zeros[:], 0.0)
+        unread = ring_banks.tile([P, K_PASS], F32, tag="ring")
+        for repeat in range(WARM_UP):
+            nc.tensor.matmul(out=unread[:], lhsT=zeros[:, 0:P], rhs=zeros[:], start=True, stop=True)
 
         kT_sb = keep.tile([P, N], BF16)
 
@@ -244,7 +251,7 @@ def tile_nsa_pa_t_kernel(tc, queries, comp_k, values, gate_cmp, out):
                 place = 1
             pair_of[i] = grouped
             halves = flipped_of[i][:].rearrange("p (g u) t -> p g t u", u=2)
-            if TILES - 3 <= i <= TILES - 2 or (i % 16 == 11 and in_pair(i)):
+            if TILES - 3 <= i <= TILES - 2 or i % 32 == 11:
                 nc.vector.tensor_copy(out=grouped[:, place].bitcast(F32), in_=halves)
             else:
                 nc.scalar.copy(out=grouped[:, place].bitcast(F32), in_=halves)

@@ -42,7 +42,7 @@ BLOCKS_A_CHUNK = N // V_CHUNKS
 CHUNKS_A_PASS = V_CHUNKS // PASSES
 V_FIRST_STEP = 1
 V_FIRST_MX = V_FIRST_STEP + V_CHUNKS // 2 + 1
-WARM_UP = 4
+WARM_UP = 12
 V_TILE = TILES
 
 FLOPS = 2 * 2 * T * N * D
@@ -69,6 +69,8 @@ def tile_nsa_pa_t_kernel(tc, queries, comp_k, values, gate_cmp, out):
         nc.sync.dma_start(out=q_sb[:, GROUP:Q_LOAD, :], in_=q_view[:, GROUP:Q_LOAD, :])
         gate_sb = keep.tile([P, TILES], BF16)
         nc.sync.dma_start(out=gate_sb[:], in_=gate_cmp[0].rearrange("(p c) -> p c", c=TILES))
+        gate_f32 = keep.tile([P, TILES], F32)
+        nc.gpsimd.tensor_copy(out=gate_f32[:], in_=gate_sb[:])
         v_sb = keep.tile([P, V_CHUNKS, V_ROWS, D], BF16)
         v_view = values[0].rearrange("(s r x) d -> r s x d", s=V_CHUNKS, x=V_ROWS)
         for g in range(PASSES):
@@ -77,6 +79,8 @@ def tile_nsa_pa_t_kernel(tc, queries, comp_k, values, gate_cmp, out):
         for first in range(Q_LOAD, TILES, Q_LOAD):
             nc.sync.dma_start(out=q_sb[:, first : first + Q_LOAD, :], in_=q_view[:, first : first + Q_LOAD, :])
 
+        zeros = keep.tile([P, P], BF16)
+        nc.vector.memset(zeros[:], 0.0)
         identity = keep.tile([P, P], BF16)
         make_identity(nc, identity[:])
         identity_f32 = keep.tile([P, P], F32)
@@ -85,11 +89,9 @@ def tile_nsa_pa_t_kernel(tc, queries, comp_k, values, gate_cmp, out):
         nc.vector.memset(warm[:], 0.0)
         nc.scalar.activation(out=warm[:], in_=warm[:], func=EXP)
 
-        zeros = keep.tile([P, K_PASS], BF16)
-        nc.vector.memset(zeros[:], 0.0)
         unread = ring_banks.tile([P, K_PASS], F32, tag="ring")
         for repeat in range(WARM_UP):
-            nc.tensor.matmul(out=unread[:], lhsT=zeros[:, 0:P], rhs=zeros[:], start=True, stop=True)
+            nc.tensor.matmul(out=unread[:, 0:P], lhsT=zeros[:], rhs=zeros[:], start=True, stop=True)
 
         kT_sb = keep.tile([P, N], BF16)
 
@@ -291,18 +293,20 @@ def tile_nsa_pa_t_kernel(tc, queries, comp_k, values, gate_cmp, out):
             factor = small.tile([P, FACTOR_BATCH], F32)
             nc.vector.tensor_reduce(out=factor[:, 0:count], in_=row_sums[:, tiles, :], axis=X_AXIS, op=ALU.add)
             nc.vector.reciprocal(out=factor[:, 0:count], in_=factor[:, 0:count])
-            nc.vector.tensor_tensor(out=factor[:, 0:count], in0=factor[:, 0:count], in1=gate_sb[:, tiles], op=ALU.mult)
             for group_first in range(first, first + count, GROUP):
                 factor_of[group_first] = factor[:, group_first - first : group_first - first + GROUP]
 
         def scale_and_store(first, count):
             out_sb = stream.tile([P, GROUP, D], F32)
-            nc.vector.tensor_tensor(
-                out=out_sb[:, 0:count, :],
-                in0=out_of[first][:, 0:count, :],
-                in1=factor_of[first][:, 0:count].unsqueeze(2).to_broadcast([P, count, D]),
-                op=ALU.mult,
-            )
+            for c in range(count):
+                nc.vector.tensor_scalar(
+                    out=out_sb[:, c, :],
+                    in0=out_of[first][:, c, :],
+                    scalar1=factor_of[first][:, c : c + 1],
+                    scalar2=gate_f32[:, first + c : first + c + 1],
+                    op0=ALU.mult,
+                    op1=ALU.mult,
+                )
             nc.sync.dma_start(out=out_view[:, first : first + count, :], in_=out_sb[:, 0:count, :])
 
         runs = [(first, GROUP) for first in range(0, TILES - GROUP, GROUP)]

@@ -69,8 +69,6 @@ def tile_nsa_pa_t_kernel(tc, queries, comp_k, values, gate_cmp, out):
         nc.sync.dma_start(out=q_sb[:, GROUP:Q_LOAD, :], in_=q_view[:, GROUP:Q_LOAD, :])
         gate_sb = keep.tile([P, TILES], BF16)
         nc.sync.dma_start(out=gate_sb[:], in_=gate_cmp[0].rearrange("(p c) -> p c", c=TILES))
-        gate_f32 = keep.tile([P, TILES], F32)
-        nc.gpsimd.tensor_copy(out=gate_f32[:], in_=gate_sb[:])
         v_sb = keep.tile([P, V_CHUNKS, V_ROWS, D], BF16)
         v_view = values[0].rearrange("(s r x) d -> r s x d", s=V_CHUNKS, x=V_ROWS)
         for g in range(PASSES):
@@ -95,14 +93,16 @@ def tile_nsa_pa_t_kernel(tc, queries, comp_k, values, gate_cmp, out):
 
         kT_sb = keep.tile([P, N], BF16)
 
-        def transpose_keys(g, copy):
-            kT_ps = ring_banks.tile([P, PACK, P], BF16, tag="ring")
-            for j in range(PACK):
-                nc.tensor.transpose(kT_ps[:, j, :], k_sb[:, g, j, :], identity[:])
-            copy(
-                out=kT_sb[:, g * K_PASS : (g + 1) * K_PASS].rearrange("d (u p h) -> d u p h", u=2, h=2),
-                in_=kT_ps[:].rearrange("d (u h) p -> d u p h", u=2),
-            )
+        def transpose_keys(g, copies):
+            for u, copy in enumerate(copies):
+                kT_ps = ring_banks.tile([P, 2, P], BF16, tag="ring")
+                for h in range(2):
+                    nc.tensor.transpose(kT_ps[:, h, :], k_sb[:, g, 2 * u + h, :], identity[:])
+                half = slice(g * K_PASS + u * K_PASS // 2, g * K_PASS + (u + 1) * K_PASS // 2)
+                copy(
+                    out=kT_sb[:, half].rearrange("d (p h) -> d p h", h=2),
+                    in_=kT_ps[:].rearrange("d h p -> d p h"),
+                )
 
         pair_sum = keep.tile([P, BLOCKS_A_CHUNK], BF16)
         column_pairs = identity[:].rearrange("r (c two) -> r c two", two=2)
@@ -253,7 +253,7 @@ def tile_nsa_pa_t_kernel(tc, queries, comp_k, values, gate_cmp, out):
                 place = 1
             pair_of[i] = grouped
             halves = flipped_of[i][:].rearrange("p (g u) t -> p g t u", u=2)
-            if TILES - 3 <= i <= TILES - 2 or i % 32 == 11:
+            if TILES - 3 <= i <= TILES - 2 or (i % 16 == 11 and i < TILES - 16):
                 nc.vector.tensor_copy(out=grouped[:, place].bitcast(F32), in_=halves)
             else:
                 nc.scalar.copy(out=grouped[:, place].bitcast(F32), in_=halves)
@@ -293,20 +293,18 @@ def tile_nsa_pa_t_kernel(tc, queries, comp_k, values, gate_cmp, out):
             factor = small.tile([P, FACTOR_BATCH], F32)
             nc.vector.tensor_reduce(out=factor[:, 0:count], in_=row_sums[:, tiles, :], axis=X_AXIS, op=ALU.add)
             nc.vector.reciprocal(out=factor[:, 0:count], in_=factor[:, 0:count])
+            nc.vector.tensor_tensor(out=factor[:, 0:count], in0=factor[:, 0:count], in1=gate_sb[:, tiles], op=ALU.mult)
             for group_first in range(first, first + count, GROUP):
                 factor_of[group_first] = factor[:, group_first - first : group_first - first + GROUP]
 
         def scale_and_store(first, count):
             out_sb = stream.tile([P, GROUP, D], F32)
-            for c in range(count):
-                nc.vector.tensor_scalar(
-                    out=out_sb[:, c, :],
-                    in0=out_of[first][:, c, :],
-                    scalar1=factor_of[first][:, c : c + 1],
-                    scalar2=gate_f32[:, first + c : first + c + 1],
-                    op0=ALU.mult,
-                    op1=ALU.mult,
-                )
+            nc.vector.tensor_tensor(
+                out=out_sb[:, 0:count, :],
+                in0=out_of[first][:, 0:count, :],
+                in1=factor_of[first][:, 0:count].unsqueeze(2).to_broadcast([P, count, D]),
+                op=ALU.mult,
+            )
             nc.sync.dma_start(out=out_view[:, first : first + count, :], in_=out_sb[:, 0:count, :])
 
         runs = [(first, GROUP) for first in range(0, TILES - GROUP, GROUP)]
@@ -327,15 +325,15 @@ def tile_nsa_pa_t_kernel(tc, queries, comp_k, values, gate_cmp, out):
             mx_step = max(last + behind, V_FIRST_MX + 2 * number)
             passes_in.setdefault(mx_step, []).append((first, count))
             stores_in.setdefault(mx_step + 1, []).append((first, count))
-        transpose_keys(0, nc.vector.tensor_copy)
+        transpose_keys(0, (nc.vector.tensor_copy, nc.scalar.copy))
         transpose_queries(0, 0, 1)
         copy_queries(0, 0, 1)
-        transpose_keys(1, nc.scalar.copy)
+        transpose_keys(1, (nc.scalar.copy, nc.vector.tensor_copy))
         scores(0)
         transpose_queries(0, 1, GROUP - 1)
         copy_queries(0, 1, GROUP - 1)
         scores(1)
-        for step in range(-Q_COPY_AHEAD + 1, max(stores_in) + 1):
+        def pipeline_step(step):
             if exists(step + MAX_AHEAD):
                 row_maximum(step + MAX_AHEAD)
             for first, count in stores_in.get(step, []):
@@ -376,3 +374,9 @@ def tile_nsa_pa_t_kernel(tc, queries, comp_k, values, gate_cmp, out):
                 transpose_queries((step + Q_TRANSPOSE_AHEAD) // GROUP)
             for first, count in passes_in.get(step, []):
                 weighted_sums(first, count)
+
+        with tc.manual_schedule(engines={mybir.EngineType.DVE}):
+            for step in range(-Q_COPY_AHEAD + 1, 1):
+                pipeline_step(step)
+        for step in range(1, max(stores_in) + 1):
+            pipeline_step(step)

@@ -31,11 +31,11 @@ SCALE = D ** -0.5
 SCORE_BANKS = 6
 PSUM_BANKS = 8
 
-MAX_AHEAD = 1
+MAX_AHEAD = 2
 COPY_BEHIND = 1
 QUANTISE_BEHIND = 2
-Q_TRANSPOSE_AHEAD = 5
-Q_COPY_AHEAD = 4
+Q_TRANSPOSE_AHEAD = 6
+Q_COPY_AHEAD = 5
 V_CHUNKS = 16
 V_ROWS = 4
 BLOCKS_A_CHUNK = N // V_CHUNKS

@@ -10,6 +10,7 @@ U8 = mybir.dt.uint8
 FP8X4 = mybir.dt.float8_e4m3fn_x4
 ALU = mybir.AluOpType
 EXP = mybir.ActivationFunctionType.Exp
+COPY = mybir.ActivationFunctionType.Copy
 X_AXIS = mybir.AxisListType.X
 
 P = 128
@@ -24,6 +25,7 @@ TILES = T // P
 GROUP = 4
 GROUPS = TILES // GROUP
 Q_LOAD = 8
+EARLY_GROUPS = 3
 FACTOR_BATCH = 2 * GROUP
 SCALE = D ** -0.5
 
@@ -66,7 +68,8 @@ def tile_nsa_pa_t_kernel(tc, queries, comp_k, values, gate_cmp, out):
         nc.sync.dma_start(out=q_sb[:, 0:1, :], in_=q_view[:, 0:1, :])
         nc.sync.dma_start(out=k_sb[:, 1], in_=k_view[:, 1])
         nc.sync.dma_start(out=q_sb[:, 1:GROUP, :], in_=q_view[:, 1:GROUP, :])
-        nc.sync.dma_start(out=q_sb[:, GROUP:Q_LOAD, :], in_=q_view[:, GROUP:Q_LOAD, :])
+        early = slice(GROUP, EARLY_GROUPS * GROUP)
+        nc.sync.dma_start(out=q_sb[:, early, :], in_=q_view[:, early, :])
         gate_sb = keep.tile([P, TILES], BF16)
         nc.sync.dma_start(out=gate_sb[:], in_=gate_cmp[0].rearrange("(p c) -> p c", c=TILES))
         v_sb = keep.tile([P, V_CHUNKS, V_ROWS, D], BF16)
@@ -74,8 +77,9 @@ def tile_nsa_pa_t_kernel(tc, queries, comp_k, values, gate_cmp, out):
         for g in range(PASSES):
             chunks = slice(g * CHUNKS_A_PASS, (g + 1) * CHUNKS_A_PASS)
             nc.sync.dma_start(out=v_sb[:, chunks], in_=v_view[:, chunks])
-        for first in range(Q_LOAD, TILES, Q_LOAD):
-            nc.sync.dma_start(out=q_sb[:, first : first + Q_LOAD, :], in_=q_view[:, first : first + Q_LOAD, :])
+        for first in range(EARLY_GROUPS * GROUP, TILES, Q_LOAD):
+            some = slice(first, min(first + Q_LOAD, TILES))
+            nc.sync.dma_start(out=q_sb[:, some, :], in_=q_view[:, some, :])
 
         zeros = keep.tile([P, P], BF16)
         nc.vector.memset(zeros[:], 0.0)
@@ -138,7 +142,7 @@ def tile_nsa_pa_t_kernel(tc, queries, comp_k, values, gate_cmp, out):
                 qT = stream.tile([P, GROUP, P], BF16)
                 qT_of[group] = qT
             part = slice(first, first + count)
-            if group == 0:
+            if group < EARLY_GROUPS:
                 nc.scalar.copy(out=qT_of[group][:, part, :], in_=qT_ps_of[group][:, part, :])
             else:
                 nc.vector.tensor_copy(out=qT_of[group][:, part, :], in_=qT_ps_of[group][:, part, :])
@@ -299,12 +303,21 @@ def tile_nsa_pa_t_kernel(tc, queries, comp_k, values, gate_cmp, out):
 
         def scale_and_store(first, count):
             out_sb = stream.tile([P, GROUP, D], F32)
-            nc.vector.tensor_tensor(
-                out=out_sb[:, 0:count, :],
-                in0=out_of[first][:, 0:count, :],
-                in1=factor_of[first][:, 0:count].unsqueeze(2).to_broadcast([P, count, D]),
-                op=ALU.mult,
-            )
+            if first == TILES - GROUP:
+                for c in range(count):
+                    nc.scalar.activation(
+                        out=out_sb[:, c, :],
+                        in_=out_of[first][:, c, :],
+                        func=COPY,
+                        scale=factor_of[first][:, c : c + 1],
+                    )
+            else:
+                nc.vector.tensor_tensor(
+                    out=out_sb[:, 0:count, :],
+                    in0=out_of[first][:, 0:count, :],
+                    in1=factor_of[first][:, 0:count].unsqueeze(2).to_broadcast([P, count, D]),
+                    op=ALU.mult,
+                )
             nc.sync.dma_start(out=out_view[:, first : first + count, :], in_=out_sb[:, 0:count, :])
 
         runs = [(first, GROUP) for first in range(0, TILES - GROUP, GROUP)]
@@ -333,6 +346,9 @@ def tile_nsa_pa_t_kernel(tc, queries, comp_k, values, gate_cmp, out):
         transpose_queries(0, 1, GROUP - 1)
         copy_queries(0, 1, GROUP - 1)
         scores(1)
+        for group in range(1, EARLY_GROUPS):
+            transpose_queries(group)
+            copy_queries(group)
         def pipeline_step(step):
             if exists(step + MAX_AHEAD):
                 row_maximum(step + MAX_AHEAD)
@@ -368,9 +384,9 @@ def tile_nsa_pa_t_kernel(tc, queries, comp_k, values, gate_cmp, out):
                 copy_out(V_TILE)
             if step == V_FIRST_STEP + V_CHUNKS // 2 + 1:
                 quantise(V_TILE)
-            if exists(step + Q_COPY_AHEAD) and (step + Q_COPY_AHEAD) % GROUP == 0:
+            if EARLY_GROUPS * GROUP <= step + Q_COPY_AHEAD < TILES and (step + Q_COPY_AHEAD) % GROUP == 0:
                 copy_queries((step + Q_COPY_AHEAD) // GROUP)
-            if exists(step + Q_TRANSPOSE_AHEAD) and (step + Q_TRANSPOSE_AHEAD) % GROUP == 0:
+            if EARLY_GROUPS * GROUP <= step + Q_TRANSPOSE_AHEAD < TILES and (step + Q_TRANSPOSE_AHEAD) % GROUP == 0:
                 transpose_queries((step + Q_TRANSPOSE_AHEAD) // GROUP)
             for first, count in passes_in.get(step, []):
                 weighted_sums(first, count)

from contextlib import ExitStack

import concourse.mybir as mybir
from concourse.masks import make_identity

BF16 = mybir.dt.bfloat16
F32 = mybir.dt.float32
U32 = mybir.dt.uint32
U8 = mybir.dt.uint8
FP8X4 = mybir.dt.float8_e4m3fn_x4
ALU = mybir.AluOpType
EXP = mybir.ActivationFunctionType.Exp
COPY = mybir.ActivationFunctionType.Copy
X_AXIS = mybir.AxisListType.X

P = 128
T = 8192
D = 128
N = 1024
BS = 8
PACK = 4
K_PASS = P * PACK
PASSES = N // K_PASS
TILES = T // P
GROUP = 4
GROUPS = TILES // GROUP
Q_LOAD = 8
EARLY_GROUPS = 3
FACTOR_BATCH = 2 * GROUP
SCALE = D ** -0.5


SCORE_BANKS = 6
PSUM_BANKS = 8

MAX_AHEAD = 2
COPY_BEHIND = 1
QUANTISE_BEHIND = 2
Q_TRANSPOSE_AHEAD = 6
Q_COPY_AHEAD = 5
V_CHUNKS = 16
V_ROWS = 4
BLOCKS_A_CHUNK = N // V_CHUNKS
CHUNKS_A_PASS = V_CHUNKS // PASSES
V_FIRST_STEP = 1
V_FIRST_MX = V_FIRST_STEP + V_CHUNKS // 2 + 1
WARM_UP = 12
V_TILE = TILES

FLOPS = 2 * 2 * T * N * D


def tile_nsa_pa_t_kernel(tc, queries, comp_k, values, gate_cmp, out):
    nc = tc.nc
    q_view = queries[0].rearrange("(p c) d -> p c d", c=TILES)
    out_view = out[0].rearrange("(p c) d -> p c d", c=TILES)

    with ExitStack() as ctx:
        keep = ctx.enter_context(tc.tile_pool(name="keep", bufs=1))
        small = ctx.enter_context(tc.tile_pool(name="small", bufs=4))
        stream = ctx.enter_context(tc.tile_pool(name="stream", bufs=4))
        ring_banks = ctx.enter_context(tc.psum_pool(name="ring_banks", bufs=PSUM_BANKS))

        k_sb = keep.tile([P, PASSES, PACK, D], BF16)
        k_view = comp_k[0].rearrange("(g p j) d -> p g j d", g=PASSES, j=PACK)
        q_sb = keep.tile([P, TILES, D], BF16)
        nc.sync.dma_start(out=k_sb[:, 0], in_=k_view[:, 0])
        nc.sync.dma_start(out=q_sb[:, 0:1, :], in_=q_view[:, 0:1, :])
        nc.sync.dma_start(out=k_sb[:, 1], in_=k_view[:, 1])
        nc.sync.dma_start(out=q_sb[:, 1:GROUP, :], in_=q_view[:, 1:GROUP, :])
        early = slice(GROUP, EARLY_GROUPS * GROUP)
        nc.sync.dma_start(out=q_sb[:, early, :], in_=q_view[:, early, :])
        gate_sb = keep.tile([P, TILES], BF16)
        nc.sync.dma_start(out=gate_sb[:], in_=gate_cmp[0].rearrange("(p c) -> p c", c=TILES))
        v_sb = keep.tile([P, V_CHUNKS, V_ROWS, D], BF16)
        v_view = values[0].rearrange("(s r x) d -> r s x d", s=V_CHUNKS, x=V_ROWS)
        for g in range(PASSES):
            chunks = slice(g * CHUNKS_A_PASS, (g + 1) * CHUNKS_A_PASS)
            nc.sync.dma_start(out=v_sb[:, chunks], in_=v_view[:, chunks])
        for first in range(EARLY_GROUPS * GROUP, TILES, Q_LOAD):
            some = slice(first, min(first + Q_LOAD, TILES))
            nc.sync.dma_start(out=q_sb[:, some, :], in_=q_view[:, some, :])

        zeros = keep.tile([P, P], BF16)
        nc.vector.memset(zeros[:], 0.0)
        identity = keep.tile([P, P], BF16)
        make_identity(nc, identity[:])
        identity_f32 = keep.tile([P, P], F32)
        make_identity(nc, identity_f32[:])
        warm = keep.tile([P, 1], F32)
        nc.vector.memset(warm[:], 0.0)
        nc.scalar.activation(out=warm[:], in_=warm[:], func=EXP)

        unread = ring_banks.tile([P, K_PASS], F32, tag="ring")
        for repeat in range(WARM_UP):
            nc.tensor.matmul(out=unread[:, 0:P], lhsT=zeros[:], rhs=zeros[:], start=True, stop=True)

        kT_sb = keep.tile([P, N], BF16)

        def transpose_keys(g, copies):
            for u, copy in enumerate(copies):
                kT_ps = ring_banks.tile([P, 2, P], BF16, tag="ring")
                for h in range(2):
                    nc.tensor.transpose(kT_ps[:, h, :], k_sb[:, g, 2 * u + h, :], identity[:])
                half = slice(g * K_PASS + u * K_PASS // 2, g * K_PASS + (u + 1) * K_PASS // 2)
                copy(
                    out=kT_sb[:, half].rearrange("d (p h) -> d p h", h=2),
                    in_=kT_ps[:].rearrange("d h p -> d p h"),
                )

        pair_sum = keep.tile([P, BLOCKS_A_CHUNK], BF16)
        column_pairs = identity[:].rearrange("r (c two) -> r c two", two=2)
        nc.vector.tensor_tensor(out=pair_sum[:], in0=column_pairs[:, :, 0], in1=column_pairs[:, :, 1], op=ALU.add)
        v_codes = keep.tile([P, PASSES * D], U32, align_bytes=64)
        v_scales = keep.tile([P, PASSES * D], U8, align_bytes=64)

        e_codes = keep.tile([P, TILES, PASSES * P], U32, align_bytes=64)
        e_scales = keep.tile([P, TILES, PASSES * P], U8, align_bytes=64)
        row_sums = keep.tile([P, TILES, PASSES], F32)
        qT_ps_of = {}
        qT_of = {}
        scores_of = {}
        neg_max_of = {}
        e_of = {}
        flipped_of = {}
        grouped_of = {}
        out_of = {}
        factor_of = {}
        v_sums_of = {}

        def exists(tile_index):
            return 0 <= tile_index < TILES

        def transpose_queries(group, first=0, count=GROUP):
            qT_ps = ring_banks.tile([P, GROUP, P], BF16, tag="ring")
            for c in range(first, first + count):
                nc.tensor.transpose(qT_ps[:, c, :], q_sb[:, group * GROUP + c, :], identity[:])
            qT_ps_of[group] = qT_ps

        def copy_queries(group, first=0, count=GROUP):
            if first == 0:
                qT = stream.tile([P, GROUP, P], BF16)
                qT_of[group] = qT
            part = slice(first, first + count)
            if group < EARLY_GROUPS:
                nc.scalar.copy(out=qT_of[group][:, part, :], in_=qT_ps_of[group][:, part, :])
            else:
                nc.vector.tensor_copy(out=qT_of[group][:, part, :], in_=qT_ps_of[group][:, part, :])

        def scores(bank_number):
            i, g = divmod(bank_number, PASSES)
            if exists(i) and (i, g) not in scores_of:
                bank = ring_banks.tile([P, K_PASS], F32, tag="ring")
                nc.tensor.matmul(
                    out=bank[:],
                    lhsT=qT_of[i // GROUP][:, i % GROUP, :],
                    rhs=kT_sb[:, g * K_PASS : (g + 1) * K_PASS],
                    start=True,
                    stop=True,
                )
                scores_of[(i, g)] = bank

        def row_maximum(i):
            bank_max = small.tile([P, PASSES], F32)
            for g in range(PASSES):
                nc.vector.tensor_reduce(out=bank_max[:, g : g + 1], in_=scores_of[(i, g)][:], axis=X_AXIS, op=ALU.max)
            neg_max = small.tile([P, 1], F32)
            nc.vector.tensor_scalar(
                out=neg_max[:],
                in0=bank_max[:, 0:1],
                scalar1=bank_max[:, 1:2],
                scalar2=-SCALE,
                op0=ALU.max,
                op1=ALU.mult,
            )
            neg_max_of[i] = neg_max

        def exponential(i, g):
            if g == 0:
                e = stream.tile([P, N], BF16)
                e_of[i] = e
            nc.scalar.activation(
                out=e_of[i][:, g * K_PASS : (g + 1) * K_PASS],
                in_=scores_of[(i, g)][:],
                func=EXP,
                bias=neg_max_of[i][:],
                scale=SCALE,
                accum_out=row_sums[:, i, g : g + 1],
            )

        def sum_blocks(s):
            g, place = divmod(s, CHUNKS_A_PASS)
            if place == 0:
                v_sums = ring_banks.tile([P, K_PASS], F32, tag="ring")
                v_sums_of[g] = v_sums
            for x in range(V_ROWS):
                nc.tensor.matmul(
                    out=v_sums_of[g][:, place * BLOCKS_A_CHUNK : (place + 1) * BLOCKS_A_CHUNK],
                    lhsT=v_sb[:, s, x, :],
                    rhs=pair_sum[:],
                    start=(x == 0),
                    stop=(x == V_ROWS - 1),
                )

        def round_means(g):
            if g == 0:
                means = stream.tile([P, N], BF16, tag="e")
                e_of[V_TILE] = means
            nc.vector.tensor_scalar(
                out=e_of[V_TILE][:, g * K_PASS : (g + 1) * K_PASS].rearrange("d (u p h) -> d u p h", u=2, h=2),
                in0=v_sums_of[g][:].rearrange("d (p u h) -> d u p h", u=2, h=2),
                scalar1=1.0 / BS,
                scalar2=None,
                op0=ALU.mult,
            )

        pair_of = {}

        def in_pair(i):
            return i < TILES - GROUP

        def in_halves(i):
            return i == TILES - 1

        def transpose_e(i, g):
            if g == 0 or in_halves(i):
                flipped = ring_banks.tile([P, PASSES * 2, P], F32, tag="ring")
                flipped_of[(i, g) if in_halves(i) else i] = flipped
            bank = flipped_of[(i, g) if in_halves(i) else i]
            words = e_of[i][:].bitcast(F32)
            for a in range(g * 2, (g + 1) * 2):
                nc.tensor.transpose(bank[:, a, :], words[:, a * P : (a + 1) * P], identity_f32[:])

        def copy_out_half(i, g):
            if g == 0:
                grouped = stream.tile([P, PASSES, P, PACK], BF16, align_bytes=64)
                grouped_of[i] = grouped
            halves = flipped_of[(i, g)][:, g * 2 : (g + 1) * 2, :].rearrange("p u t -> p t u")
            if g == 0:
                nc.vector.tensor_copy(out=grouped_of[i][:, g].bitcast(F32), in_=halves)
            else:
                nc.scalar.copy(out=grouped_of[i][:, g].bitcast(F32), in_=halves)

        def quantise_half(i, g):
            nc.vector.quantize_mx(
                out=e_codes[:, i, g * P : (g + 1) * P].bitcast(FP8X4),
                scales=e_scales[:, i, g * P : (g + 1) * P],
                in_=grouped_of[i][:, g].rearrange("p t j -> p (t j)"),
            )

        def copy_out(i):
            if i % 2 == 0 or not in_pair(i):
                grouped = stream.tile([P, 2, PASSES, P, PACK], BF16, align_bytes=64)
                place = 0
            else:
                grouped = pair_of[i - 1]
                place = 1
            pair_of[i] = grouped
            halves = flipped_of[i][:].rearrange("p (g u) t -> p g t u", u=2)
            if TILES - 3 <= i <= TILES - 2 or (i % 16 == 11 and i < TILES - 16):
                nc.vector.tensor_copy(out=grouped[:, place].bitcast(F32), in_=halves)
            else:
                nc.scalar.copy(out=grouped[:, place].bitcast(F32), in_=halves)

        def quantise(i):
            if in_pair(i) and i % 2 == 0:
                return
            count = 2 if in_pair(i) else 1
            tiles = slice(i + 1 - count, i + 1)
            codes, scale_bytes = (v_codes[:], v_scales[:]) if i == V_TILE else (e_codes[:, tiles, :], e_scales[:, tiles, :])
            if i != V_TILE:
                codes, scale_bytes = codes.rearrange("p c w -> p (c w)"), scale_bytes.rearrange("p c w -> p (c w)")
            nc.vector.quantize_mx(
                out=codes.bitcast(FP8X4),
                scales=scale_bytes,
                in_=pair_of[i][:, 0:count].rearrange("p c g t j -> p (c g t j)"),
            )

        def weighted_sums(first, count):
            out_ps = ring_banks.tile([P, GROUP, D], F32, tag="ring")
            for c in range(count):
                i = first + c
                for g in range(PASSES):
                    nc.tensor.matmul_mx(
                        out=out_ps[:, c, :],
                        lhsT=e_codes[:, i, g * P : (g + 1) * P].bitcast(FP8X4),
                        lhsT_scale=e_scales[:, i, g * P : (g + 1) * P],
                        rhs=v_codes[:, g * D : (g + 1) * D].bitcast(FP8X4),
                        rhs_scale=v_scales[:, g * D : (g + 1) * D],
                        start=(g == 0),
                        stop=(g == PASSES - 1),
                    )
            out_of[first] = out_ps

        def factors(first, count):
            tiles = slice(first, first + count)
            factor = small.tile([P, FACTOR_BATCH], F32)
            nc.vector.tensor_reduce(out=factor[:, 0:count], in_=row_sums[:, tiles, :], axis=X_AXIS, op=ALU.add)
            nc.vector.reciprocal(out=factor[:, 0:count], in_=factor[:, 0:count])
            nc.vector.tensor_tensor(out=factor[:, 0:count], in0=factor[:, 0:count], in1=gate_sb[:, tiles], op=ALU.mult)
            for group_first in range(first, first + count, GROUP):
                factor_of[group_first] = factor[:, group_first - first : group_first - first + GROUP]

        def scale_and_store(first, count):
            out_sb = stream.tile([P, GROUP, D], F32)
            if first == TILES - GROUP:
                for c in range(count):
                    nc.scalar.activation(
                        out=out_sb[:, c, :],
                        in_=out_of[first][:, c, :],
                        func=COPY,
                        scale=factor_of[first][:, c : c + 1],
                    )
            else:
                nc.vector.tensor_tensor(
                    out=out_sb[:, 0:count, :],
                    in0=out_of[first][:, 0:count, :],
                    in1=factor_of[first][:, 0:count].unsqueeze(2).to_broadcast([P, count, D]),
                    op=ALU.mult,
                )
            nc.sync.dma_start(out=out_view[:, first : first + count, :], in_=out_sb[:, 0:count, :])

        runs = [(first, GROUP) for first in range(0, TILES - GROUP, GROUP)]
        runs.extend([(TILES - GROUP, GROUP - 1), (TILES - 1, 1)])
        BATCHED_TILES = TILES - FACTOR_BATCH
        factors_in = {}
        passes_in = {}
        stores_in = {}
        for number, (first, count) in enumerate(runs):
            last = first + count - 1
            if last < BATCHED_TILES:
                if first % FACTOR_BATCH == 0:
                    factors_in.setdefault(first + FACTOR_BATCH, []).append((first, FACTOR_BATCH))
                behind = GROUP if last == BATCHED_TILES - 1 else GROUP + 2
            else:
                factors_in.setdefault(last + 1, []).append((first, count))
                behind = QUANTISE_BEHIND
            mx_step = max(last + behind, V_FIRST_MX + 2 * number)
            passes_in.setdefault(mx_step, []).append((first, count))
            stores_in.setdefault(mx_step + 1, []).append((first, count))
        transpose_keys(0, (nc.vector.tensor_copy, nc.scalar.copy))
        transpose_queries(0, 0, 1)
        copy_queries(0, 0, 1)
        transpose_keys(1, (nc.scalar.copy, nc.vector.tensor_copy))
        scores(0)
        transpose_queries(0, 1, GROUP - 1)
        copy_queries(0, 1, GROUP - 1)
        scores(1)
        for group in range(1, EARLY_GROUPS):
            transpose_queries(group)
            copy_queries(group)
        def pipeline_step(step):
            if exists(step + MAX_AHEAD):
                row_maximum(step + MAX_AHEAD)
            for first, count in stores_in.get(step, []):
                scale_and_store(first, count)
            for g in range(PASSES):
                if exists(step):
                    exponential(step, g)
                    transpose_e(step, g)
                scores(PASSES * step + g + SCORE_BANKS)
            if in_halves(step - QUANTISE_BEHIND):
                quantise_half(step - QUANTISE_BEHIND, 1)
            elif exists(step - QUANTISE_BEHIND):
                quantise(step - QUANTISE_BEHIND)
            if in_halves(step - COPY_BEHIND):
                quantise_half(step - COPY_BEHIND, 0)
            for first, count in factors_in.get(step, []):
                factors(first, count)
            if in_halves(step - COPY_BEHIND):
                copy_out_half(step - COPY_BEHIND, 1)
            elif exists(step - COPY_BEHIND):
                copy_out(step - COPY_BEHIND)
            if in_halves(step):
                copy_out_half(step, 0)
            for s in range(2 * (step - V_FIRST_STEP), 2 * (step - V_FIRST_STEP) + 2):
                if 0 <= s < V_CHUNKS:
                    sum_blocks(s)
                    if (s + 1) % CHUNKS_A_PASS == 0:
                        round_means(s // CHUNKS_A_PASS)
            if step == V_FIRST_STEP + V_CHUNKS // 2:
                for g in range(PASSES):
                    transpose_e(V_TILE, g)
                copy_out(V_TILE)
            if step == V_FIRST_STEP + V_CHUNKS // 2 + 1:
                quantise(V_TILE)
            if EARLY_GROUPS * GROUP <= step + Q_COPY_AHEAD < TILES and (step + Q_COPY_AHEAD) % GROUP == 0:
                copy_queries((step + Q_COPY_AHEAD) // GROUP)
            if EARLY_GROUPS * GROUP <= step + Q_TRANSPOSE_AHEAD < TILES and (step + Q_TRANSPOSE_AHEAD) % GROUP == 0:
                transpose_queries((step + Q_TRANSPOSE_AHEAD) // GROUP)
            for first, count in passes_in.get(step, []):
                weighted_sums(first, count)

        with tc.manual_schedule(engines={mybir.EngineType.DVE}):
            for step in range(-Q_COPY_AHEAD + 1, 1):
                pipeline_step(step)
        for step in range(1, max(stores_in) + 1):
            pipeline_step(step)
